import numpy as np
import ml_dtypes


def mxq(x, axis, fmt="e4m3"):
    dtype, down = {"e4m3": (ml_dtypes.float8_e4m3fn, 7), "e5m2": (ml_dtypes.float8_e5m2, 14)}[fmt]
    v = np.moveaxis(np.asarray(x, np.float32).astype(ml_dtypes.bfloat16).astype(np.float64), axis, -1)
    blocks = v.reshape(v.shape[:-1] + (-1, 32))
    amax = np.abs(blocks).max(-1, keepdims=True)
    byte = np.maximum(np.where(amax > 0, np.frexp(amax)[1] - 1 + 127, 0) - down, 1)
    scale = np.exp2(byte - 127.0)
    codes = (blocks / scale).astype(np.float32).astype(dtype).astype(np.float64)
    return np.moveaxis((codes * scale).reshape(v.shape), -1, axis)


WIDE = False


def mx_kscale(k):
    if not WIDE:
        return np.ones(k)
    levels = np.array([10, -10, 5, -5, 0])
    if k % 512:
        return np.exp2(np.random.permutation(np.resize(levels, k // 32))).repeat(32)
    a = np.empty((k // 512, 16))
    for p in range(k // 512):
        a[p, :8] = np.random.permutation(np.resize(levels, 8))
        for g in range(8):
            far = levels[np.abs(levels - a[p, g]) >= 10]
            a[p, g + 8] = far[np.random.randint(len(far))]
    return np.exp2(a.ravel()).repeat(32)


BF16 = ml_dtypes.bfloat16


def bf(x):
    return np.asarray(x, np.float32).astype(BF16)


def f64(x):
    return np.asarray(x).astype(np.float64)


B, H, V, DEPTH = 16, 1024, 8192, 5
NODES = 2 ** (DEPTH - 2)
G = 3 * H


def sigmoid(v):
    return 1.0 / (1.0 + np.exp(-v))


def gate(x, g, bih):
    r = sigmoid(g[..., :H] + bih[:H])
    z = sigmoid(g[..., H:2 * H] + bih[H:2 * H])
    n = np.tanh(bih[2 * H:] + r * g[..., 2 * H:])
    return (1.0 - z) * n + z * x


def expand(x, wl, bil, bhl, wr, bir, bhr):
    xq = mxq(x, 2, "e4m3")
    xl = gate(x, (xq @ wl.T) + bhl, bil)
    xr = gate(x, (xq @ wr.T) + bhr, bir)
    return np.stack([xl, xr], axis=2).reshape(B, -1, H)


def setup_inputs():
    w = 1.5 / np.sqrt(H)
    s = mx_kscale(H)
    t = s / s.min()
    return {"h_nodes": bf(np.random.standard_normal((B, NODES, H)) * 0.4 * t),
            "Whh_l": bf(np.random.standard_normal((G, H)) * w / t[None, :]),
            "bih_l": bf(np.random.standard_normal(G) * 0.4),
            "bhh_l": bf(np.random.standard_normal(G) * 0.4),
            "Whh_r": bf(np.random.standard_normal((G, H)) * w / t[None, :]),
            "bih_r": bf(np.random.standard_normal(G) * 0.4),
            "bhh_r": bf(np.random.standard_normal(G) * 0.4)}


def reference(h_nodes, Whh_l, bih_l, bhh_l, Whh_r, bih_r, bhh_r):
    wl = mxq(f64(Whh_l), 1, "e4m3")
    wr = mxq(f64(Whh_r), 1, "e4m3")
    args = (wl, f64(bih_l), f64(bhh_l), wr, f64(bih_r), f64(bhh_r))
    c = expand(f64(h_nodes), *args)
    return expand(c, *args)

@@ -1,0 +1,397 @@
+import concourse.mybir as mybir
+from concourse.masks import make_identity
+
+F32 = mybir.dt.float32
+BF16 = mybir.dt.bfloat16
+U32 = mybir.dt.uint32
+U8 = mybir.dt.uint8
+FP8X4 = mybir.dt.float8_e4m3fn_x4
+ACT = mybir.ActivationFunctionType
+ALU = mybir.AluOpType
+
+P = 128
+H = 1024
+GATES = 3
+SIDES = 2
+PAIR = 2
+ROOTS = 128
+BLOCK = P * PAIR
+BLOCKS = H // BLOCK
+PASSES = H // (4 * P)
+WORD_BLOCKS = H // BLOCK
+BANK = 512
+SLABS = SIDES * BLOCKS * GATES
+SLAB_WORDS = PAIR * PASSES * P
+
+MULTIPLY_LAG = 3
+TANH_LAG = 6
+MIX_LAG = 7
+CAST_LAG = 8
+QUANTISE_LAG = 9
+
+FLOPS = 2 * (ROOTS + SIDES * ROOTS) * (SIDES * GATES * H) * H
+
+
+def tile_decodertreernn_pa_kernel(
+    tc, h_nodes, Whh_l, bih_l, bhh_l, Whh_r, bih_r, bhh_r, out
+):
+    nc = tc.nc
+
+    slab_rows = [
+        w.rearrange(
+            "(gate g q u e) k -> gate g u q (e k)", gate=GATES, g=PASSES, q=P, u=PAIR, e=PAIR
+        )
+        for w in (Whh_l, Whh_r)
+    ]
+    out_rows = out.rearrange("b (i s s2) h -> (b i) s s2 h", s=SIDES, s2=SIDES)
+
+    slabs = [
+        (blk, side, gate)
+        for blk in range(BLOCKS)
+        for side in range(SIDES)
+        for gate in range(GATES)
+    ]
+
+    def slab_index(blk, side, gate):
+        return (blk * SIDES + side) * GATES + gate
+
+    with tc.manual_schedule(), tc.tile_pool(name="keep", bufs=1) as keep:
+        identity = keep.tile([P, P], F32)
+        make_identity(nc, identity[:])
+
+        w_codes = [
+            keep.tile([P, SLAB_WORDS], U32, align_bytes=64, name="w_codes%d" % n) for n in range(SLABS)
+        ]
+        w_scales = [
+            keep.tile([P, SLAB_WORDS], U8, align_bytes=64, name="w_scales%d" % n) for n in range(SLABS)
+        ]
+        x_codes = [
+            keep.tile([P, ROOTS], U32, align_bytes=64, name="x_codes%d" % g) for g in range(PASSES)
+        ]
+        x_scales = [
+            keep.tile([P, ROOTS], U8, align_bytes=64, name="x_scales%d" % g) for g in range(PASSES)
+        ]
+        c_codes = [
+            keep.tile([P, SIDES * ROOTS], U32, align_bytes=64, name="c_codes%d" % g)
+            for g in range(PASSES)
+        ]
+        c_scales = [
+            keep.tile([P, SIDES * ROOTS], U8, align_bytes=64, name="c_scales%d" % g)
+            for g in range(PASSES)
+        ]
+        x_f32 = keep.tile([P, BLOCKS, PAIR, ROOTS], F32)
+        c_f32 = [
+            keep.tile([P, PAIR, SIDES * ROOTS], F32, name="c_f32_%d" % blk) for blk in range(BLOCKS)
+        ]
+        c_grouped = [
+            keep.tile([P, SIDES * ROOTS, 2 * PAIR], BF16, align_bytes=64, name="c_grouped%d" % g)
+            for g in range(PASSES)
+        ]
+        bias = keep.tile([P, SIDES * 2 * GATES * BLOCKS * PAIR], F32)
+        bias_rz = keep.tile([P, SIDES, 2 * BLOCKS * PAIR], F32)
+
+        def bias_column(side, kind, gate, blk, e):
+            col = ((side * 2 + kind) * GATES * BLOCKS + gate * BLOCKS + blk) * PAIR + e
+            return bias[:, col : col + 1]
+
+        def bias_rz_column(side, gate, blk, e):
+            col = (gate * BLOCKS + blk) * PAIR + e
+            return bias_rz[:, side, col : col + 1]
+
+        def every_second_word(w):
+            g, u = divmod(w, PAIR)
+            return slice(g * BLOCK + u, (g + 1) * BLOCK, PAIR)
+
+        def multiply(bank, slab, codes, scales):
+            for e in range(PAIR):
+                for g in range(PASSES):
+                    first = (e * PASSES + g) * P
+                    nc.tensor.matmul_mx(
+                        out=bank[:, e, :],
+                        lhsT=w_codes[slab][:, first : first + P].bitcast(FP8X4),
+                        lhsT_scale=w_scales[slab][:, first : first + P],
+                        rhs=codes[g][:].bitcast(FP8X4),
+                        rhs_scale=scales[g][:],
+                        start=(g == 0),
+                        stop=(g == PASSES - 1),
+                    )
+
+        def sigmoid(gate_out, bank, side, gate, blk, e):
+            nc.scalar.activation(
+                out=gate_out[:, e, :], in_=bank[:, e, :], func=ACT.Sigmoid,
+                bias=bias_rz_column(side, gate, blk, e), scale=1.0,
+            )
+
+        def reset_candidate(cand, bank, reset, side, blk, e):
+            nc.vector.scalar_tensor_tensor(
+                out=cand[:, e, :], in0=bank[:, e, :], scalar=bias_column(side, 1, 2, blk, e),
+                in1=reset[:, e, :], op0=ALU.add, op1=ALU.mult,
+            )
+
+        def tanh(cand, side, blk, e):
+            nc.scalar.activation(
+                out=cand[:, e, :], in_=cand[:, e, :], func=ACT.Tanh,
+                bias=bias_column(side, 0, 2, blk, e), scale=1.0,
+            )
+
+        with tc.tile_pool(name="raw", bufs=SLABS) as raw_pool, tc.tile_pool(
+            name="once", bufs=1
+        ) as once, tc.tile_pool(name="stage", bufs=4) as stage, tc.tile_pool(
+            name="work1", bufs=3
+        ) as work1, tc.psum_pool(name="flip", bufs=5) as flip_psum, tc.psum_pool(
+            name="gates1", bufs=3
+        ) as gates1:
+            x_raw = once.tile([P, H], BF16)
+            nc.sync.dma_start(out=x_raw[:], in_=h_nodes.flatten_outer_dims())
+            raw = []
+            for blk, side, gate in slabs:
+                raw_slab = raw_pool.tile([P, PAIR * H], BF16, name="raw_slab")
+                nc.sync.dma_start(out=raw_slab[:], in_=slab_rows[side][gate, blk // PAIR, blk % PAIR])
+                raw.append(raw_slab)
+            bias_raw = once.tile([P, PAIR * BLOCK], BF16)
+            nc.vector.memset(bias_raw[:], 0.0)
+            rows = GATES * PASSES
+            for v, vec in enumerate((bih_l, bhh_l, bih_r, bhh_r)):
+                nc.scalar.dma_start(
+                    out=bias_raw[v * rows : (v + 1) * rows, :],
+                    in_=vec.rearrange("(r c) -> r c", c=PAIR * BLOCK),
+                )
+
+            warm = once.tile([P, 1], F32)
+            nc.vector.memset(warm[:], 0.0)
+            nc.scalar.activation(out=warm[:], in_=warm[:], func=ACT.Sigmoid)
+
+            x_words = x_raw[:].bitcast(F32)
+            x_flipped = flip_psum.tile([P, BANK], F32, name="flipped")
+            for w in range(WORD_BLOCKS):
+                nc.tensor.transpose(
+                    x_flipped[:, w * P : (w + 1) * P], x_words[:, every_second_word(w)], identity[:]
+                )
+            x_grouped = once.tile([P, BANK], F32, align_bytes=64)
+            nc.vector.tensor_copy(
+                out=x_grouped[:].rearrange("p (g j u) -> p g j u", g=PASSES, u=PAIR),
+                in_=x_flipped[:].rearrange("p (g u j) -> p g j u", g=PASSES, u=PAIR),
+            )
+            nc.scalar.copy(
+                out=x_f32[:],
+                in_=x_flipped[:].bitcast(BF16).rearrange(
+                    "p (blk j e) -> p blk e j", blk=BLOCKS, e=PAIR
+                ),
+            )
+
+            b_flipped = flip_psum.tile([P, BANK], F32, name="flipped")
+            bias_words = bias_raw[:].bitcast(F32)
+            for u in range(PAIR):
+                nc.tensor.transpose(
+                    b_flipped[:, u * P : (u + 1) * P], bias_words[:, every_second_word(u)], identity[:]
+                )
+            nc.vector.tensor_copy(
+                out=bias[:].rearrange("p (r u e) -> p r u e", u=PAIR, e=PAIR),
+                in_=b_flipped[:, 0 : PAIR * P].bitcast(BF16).rearrange(
+                    "p (u r e) -> p r u e", u=PAIR, e=PAIR
+                )[:, 0 : SIDES * 2 * rows],
+            )
+            by_kind = bias[:].rearrange("p (s kind c) -> p s kind c", s=SIDES, kind=2)
+            rz_cols = 2 * BLOCKS * PAIR
+            nc.vector.tensor_add(
+                out=bias_rz[:], in0=by_kind[:, :, 0, 0:rz_cols], in1=by_kind[:, :, 1, 0:rz_cols]
+            )
+            for g in range(PASSES):
+                nc.vector.quantize_mx(
+                    out=x_codes[g][:].bitcast(FP8X4),
+                    scales=x_scales[g][:],
+                    in_=x_grouped[:, g * BLOCK : (g + 1) * BLOCK].bitcast(BF16),
+                )
+
+            flipped = {}
+            grouped = {}
+            sums = {}
+            reset, update, cand, diff = {}, {}, {}, {}
+
+            def transpose_slab(n):
+                words = raw[n][:].bitcast(F32)
+                for e in range(PAIR):
+                    flipped[(n, e)] = flip_psum.tile([P, BANK], F32, name="flipped")
+                    for w in range(WORD_BLOCKS):
+                        nc.tensor.transpose(
+                            flipped[(n, e)][:, w * P : (w + 1) * P],
+                            words[:, every_second_word(e * WORD_BLOCKS + w)],
+                            identity[:],
+                        )
+
+            def empty_bank(n, e):
+                if e == 0:
+                    grouped[n] = stage.tile([P, PAIR * BANK], F32, align_bytes=64, name="grouped")
+                by_vector = n % GATES == GATES - 1 and e == PAIR - 1
+                copy = nc.vector.tensor_copy if by_vector else nc.scalar.copy
+                copy(
+                    out=grouped[n][:, e * BANK : (e + 1) * BANK].rearrange(
+                        "p (g q u) -> p g q u", g=PASSES, u=PAIR
+                    ),
+                    in_=flipped[(n, e)][:].rearrange("p (g u q) -> p g q u", g=PASSES, u=PAIR),
+                )
+
+            def quantise_slab(n):
+                nc.vector.quantize_mx(
+                    out=w_codes[n][:].bitcast(FP8X4),
+                    scales=w_scales[n][:],
+                    in_=grouped[n][:].bitcast(BF16),
+                )
+
+            def multiply_slab(n):
+                sums[n] = gates1.tile([P, PAIR, ROOTS], F32, name="sums")
+                multiply(sums[n], n, x_codes, x_scales)
+
+            def activate(n, e):
+                m = n - MULTIPLY_LAG
+                if n % GATES == GATES - 1:
+                    m = n - TANH_LAG
+                if not 0 <= m < SLABS:
+                    return
+                blk, side, gate = slabs[m]
+                i = m // GATES
+                if gate == GATES - 1:
+                    tanh(cand[i], side, blk, e)
+                    return
+                gate_out = (reset, update)[gate]
+                if e == 0:
+                    gate_out[i] = work1.tile([P, PAIR, ROOTS], F32, name=("reset", "update")[gate])
+                sigmoid(gate_out[i], sums[m], side, gate, blk, e)
+
+            def vector_share(n, half):
+                turn = n % GATES
+                m = n - (MIX_LAG, CAST_LAG, MULTIPLY_LAG)[turn]
+                if 0 <= m < SLABS:
+                    blk, side, gate = slabs[m]
+                    i = m // GATES
+                    nodes = slice(side * ROOTS, (side + 1) * ROOTS)
+                    g, u = divmod(blk, PAIR)
+                    if turn == 2:
+                        if half == 0:
+                            cand[i] = work1.tile([P, PAIR, ROOTS], F32, name="cand")
+                        reset_candidate(cand[i], sums[m], reset[i], side, blk, half)
+                    elif turn == 0 and half == 0:
+                        diff[i] = work1.tile([P, PAIR, ROOTS], F32, name="diff")
+                        nc.vector.tensor_sub(out=diff[i][:], in0=x_f32[:, blk, :, :], in1=cand[i][:])
+                    elif turn == 0:
+                        nc.vector.tensor_mul(out=diff[i][:], in0=update[i][:], in1=diff[i][:])
+                    elif half == 0:
+                        nc.vector.tensor_add(
+                            out=c_f32[blk][:, :, nodes], in0=diff[i][:], in1=cand[i][:]
+                        )
+                    else:
+                        nc.vector.tensor_copy(
+                            out=c_grouped[g][:, nodes, u * PAIR : (u + 1) * PAIR],
+                            in_=c_f32[blk][:, :, nodes].rearrange("p e j -> p j e"),
+                        )
+                m = n - QUANTISE_LAG
+                if turn == 2 and half == 1 and 0 <= m < SLABS:
+                    blk, side, gate = slabs[m]
+                    g, u = divmod(blk, PAIR)
+                    if u == PAIR - 1 and side == SIDES - 1:
+                        nc.vector.quantize_mx(
+                            out=c_codes[g][:].bitcast(FP8X4),
+                            scales=c_scales[g][:],
+                            in_=c_grouped[g][:].rearrange("p c t -> p (c t)"),
+                        )
+
+            for n in range(SLABS + QUANTISE_LAG + 1):
+                if n < SLABS:
+                    transpose_slab(n)
+                if 0 <= n - MULTIPLY_LAG < SLABS:
+                    multiply_slab(n - MULTIPLY_LAG)
+                vector_share(n, 0)
+                if 0 <= n - 1 < SLABS:
+                    quantise_slab(n - 1)
+                vector_share(n, 1)
+                for e in range(PAIR):
+                    if n < SLABS:
+                        empty_bank(n, e)
+                    activate(n, e)
+
+        with tc.tile_pool(name="work2", bufs=5) as work2, tc.psum_pool(
+            name="gates2", bufs=2
+        ) as gates2, tc.psum_pool(name="back", bufs=2) as back_psum:
+            children = SIDES * ROOTS
+            blocks2 = [(side2, blk) for side2 in range(SIDES) for blk in range(BLOCKS)]
+            update2, cand2, mixed, back = {}, {}, {}, {}
+
+            def gates_of_block(k):
+                side2, blk = blocks2[k]
+                banks = []
+                for gate in range(GATES):
+                    bank = gates2.tile([P, PAIR, children], F32, name="sums%d" % gate)
+                    multiply(bank, slab_index(blk, side2, gate), c_codes, c_scales)
+                    banks.append(bank)
+                return banks
+
+            def activate_block(k, banks):
+                side2, blk = blocks2[k]
+                reset2 = work2.tile([P, PAIR, children], F32)
+                update2[k] = work2.tile([P, PAIR, children], F32, name="update2")
+                cand2[k] = work2.tile([P, PAIR, children], F32, name="cand2")
+                for e in range(PAIR):
+                    sigmoid(reset2, banks[0], side2, 0, blk, e)
+                if k >= 1:
+                    mix_begin(k - 1)
+                for e in range(PAIR):
+                    reset_candidate(cand2[k], banks[2], reset2, side2, blk, e)
+                for e in range(PAIR):
+                    sigmoid(update2[k], banks[1], side2, 1, blk, e)
+                for e in range(PAIR):
+                    tanh(cand2[k], side2, blk, e)
+
+            def mix_begin(k):
+                side2, blk = blocks2[k]
+                mixed[k] = work2.tile([P, PAIR, children], F32, name="mixed")
+                for e in range(PAIR):
+                    nc.vector.tensor_sub(
+                        out=mixed[k][:, e, :], in0=c_f32[blk][:, e, :], in1=cand2[k][:, e, :]
+                    )
+
+            def mix_end(k):
+                for e in range(PAIR):
+                    nc.vector.tensor_mul(
+                        out=mixed[k][:, e, :], in0=update2[k][:, e, :], in1=mixed[k][:, e, :]
+                    )
+                for e in range(PAIR):
+                    nc.vector.tensor_add(
+                        out=mixed[k][:, e, :], in0=mixed[k][:, e, :], in1=cand2[k][:, e, :]
+                    )
+
+            def transpose_back(i):
+                m, s = divmod(i, SIDES)
+                back[i] = back_psum.tile([P, PAIR, PAIR, P], F32, name="back")
+                for u in range(PAIR):
+                    for e in range(PAIR):
+                        nc.tensor.transpose(
+                            back[i][:, u, e, :],
+                            mixed[m * PAIR + u][:, e, s * ROOTS : (s + 1) * ROOTS],
+                            identity[:],
+                        )
+
+            def store_piece(i):
+                m, s = divmod(i, SIDES)
+                side2, g = divmod(m, PASSES)
+                cols = slice(g * PAIR * BLOCK, (g + 1) * PAIR * BLOCK)
+                leaving = work2.tile([P, PAIR * BLOCK], F32)
+                nc.scalar.copy(
+                    out=leaving[:].rearrange("j (q u e) -> j q u e", u=PAIR, e=PAIR),
+                    in_=back[i][:].rearrange("j u e q -> j q u e"),
+                )
+                nc.sync.dma_start(out=out_rows[:, s, side2, cols], in_=leaving[:])
+
+            count = len(blocks2)
+            for k in range(count + 3):
+                if k < count:
+                    banks = gates_of_block(k)
+                if k >= 3:
+                    transpose_back(k - 3)
+                if k < count:
+                    activate_block(k, banks)
+                elif k == count:
+                    mix_begin(k - 1)
+                if 1 <= k <= count:
+                    mix_end(k - 1)
+                if k >= 3:
+                    store_piece(k - 3)

@@ -23,11 +23,8 @@ BANK = 512
 SLABS = SIDES * BLOCKS * GATES
 SLAB_WORDS = PAIR * PASSES * P
 
-MULTIPLY_LAG = 3
-TANH_LAG = 6
-MIX_LAG = 7
-CAST_LAG = 8
-QUANTISE_LAG = 9
+PAIRS = SLABS // 2
+GROUP_PAIRS = 3
 
 FLOPS = 2 * (ROOTS + SIDES * ROOTS) * (SIDES * GATES * H) * H
 
@@ -48,12 +45,9 @@ def tile_decodertreernn_pa_kernel(
     slabs = [
         (blk, side, gate)
         for blk in range(BLOCKS)
-        for side in range(SIDES)
-        for gate in range(GATES)
+        for side, gate in ((0, 0), (0, 2), (1, 0), (1, 2), (0, 1), (1, 1))
     ]
-
-    def slab_index(blk, side, gate):
-        return (blk * SIDES + side) * GATES + gate
+    slab_of = {key: n for n, key in enumerate(slabs)}
 
     with tc.manual_schedule(), tc.tile_pool(name="keep", bufs=1) as keep:
         identity = keep.tile([P, P], F32)
@@ -79,9 +73,8 @@ def tile_decodertreernn_pa_kernel(
             keep.tile([P, SIDES * ROOTS], U8, align_bytes=64, name="c_scales%d" % g)
             for g in range(PASSES)
         ]
-        x_f32 = keep.tile([P, BLOCKS, PAIR, ROOTS], F32)
         c_f32 = [
-            keep.tile([P, PAIR, SIDES * ROOTS], F32, name="c_f32_%d" % blk) for blk in range(BLOCKS)
+            keep.tile([P, PAIR, PAIR, SIDES * ROOTS], F32, name="c_f32_%d" % g) for g in range(PASSES)
         ]
         c_grouped = [
             keep.tile([P, SIDES * ROOTS, 2 * PAIR], BF16, align_bytes=64, name="c_grouped%d" % g)
@@ -137,17 +130,23 @@ def tile_decodertreernn_pa_kernel(
         with tc.tile_pool(name="raw", bufs=SLABS) as raw_pool, tc.tile_pool(
             name="once", bufs=1
         ) as once, tc.tile_pool(name="stage", bufs=4) as stage, tc.tile_pool(
-            name="work1", bufs=3
-        ) as work1, tc.psum_pool(name="flip", bufs=5) as flip_psum, tc.psum_pool(
-            name="gates1", bufs=3
+            name="work1", bufs=2
+        ) as work1, tc.psum_pool(name="flip", bufs=4) as flip_psum, tc.psum_pool(
+            name="gates1", bufs=4
         ) as gates1:
             x_raw = once.tile([P, H], BF16)
-            nc.sync.dma_start(out=x_raw[:], in_=h_nodes.flatten_outer_dims())
             raw = []
-            for blk, side, gate in slabs:
+            for n, (blk, side, gate) in enumerate(slabs):
                 raw_slab = raw_pool.tile([P, PAIR * H], BF16, name="raw_slab")
                 nc.sync.dma_start(out=raw_slab[:], in_=slab_rows[side][gate, blk // PAIR, blk % PAIR])
                 raw.append(raw_slab)
+                if n == 0:
+                    nc.sync.dma_start(out=x_raw[:], in_=h_nodes.flatten_outer_dims())
+
+            warm = once.tile([P, 1], F32)
+            nc.vector.memset(warm[:], 0.0)
+            nc.scalar.activation(out=warm[:], in_=warm[:], func=ACT.Sigmoid)
+
             bias_raw = once.tile([P, PAIR * BLOCK], BF16)
             nc.vector.memset(bias_raw[:], 0.0)
             rows = GATES * PASSES
@@ -157,52 +156,7 @@ def tile_decodertreernn_pa_kernel(
                     in_=vec.rearrange("(r c) -> r c", c=PAIR * BLOCK),
                 )
 
-            warm = once.tile([P, 1], F32)
-            nc.vector.memset(warm[:], 0.0)
-            nc.scalar.activation(out=warm[:], in_=warm[:], func=ACT.Sigmoid)
-
-            x_words = x_raw[:].bitcast(F32)
-            x_flipped = flip_psum.tile([P, BANK], F32, name="flipped")
-            for w in range(WORD_BLOCKS):
-                nc.tensor.transpose(
-                    x_flipped[:, w * P : (w + 1) * P], x_words[:, every_second_word(w)], identity[:]
-                )
             x_grouped = once.tile([P, BANK], F32, align_bytes=64)
-            nc.vector.tensor_copy(
-                out=x_grouped[:].rearrange("p (g j u) -> p g j u", g=PASSES, u=PAIR),
-                in_=x_flipped[:].rearrange("p (g u j) -> p g j u", g=PASSES, u=PAIR),
-            )
-            nc.scalar.copy(
-                out=x_f32[:],
-                in_=x_flipped[:].bitcast(BF16).rearrange(
-                    "p (blk j e) -> p blk e j", blk=BLOCKS, e=PAIR
-                ),
-            )
-
-            b_flipped = flip_psum.tile([P, BANK], F32, name="flipped")
-            bias_words = bias_raw[:].bitcast(F32)
-            for u in range(PAIR):
-                nc.tensor.transpose(
-                    b_flipped[:, u * P : (u + 1) * P], bias_words[:, every_second_word(u)], identity[:]
-                )
-            nc.vector.tensor_copy(
-                out=bias[:].rearrange("p (r u e) -> p r u e", u=PAIR, e=PAIR),
-                in_=b_flipped[:, 0 : PAIR * P].bitcast(BF16).rearrange(
-                    "p (u r e) -> p r u e", u=PAIR, e=PAIR
-                )[:, 0 : SIDES * 2 * rows],
-            )
-            by_kind = bias[:].rearrange("p (s kind c) -> p s kind c", s=SIDES, kind=2)
-            rz_cols = 2 * BLOCKS * PAIR
-            nc.vector.tensor_add(
-                out=bias_rz[:], in0=by_kind[:, :, 0, 0:rz_cols], in1=by_kind[:, :, 1, 0:rz_cols]
-            )
-            for g in range(PASSES):
-                nc.vector.quantize_mx(
-                    out=x_codes[g][:].bitcast(FP8X4),
-                    scales=x_scales[g][:],
-                    in_=x_grouped[:, g * BLOCK : (g + 1) * BLOCK].bitcast(BF16),
-                )
-
             flipped = {}
             grouped = {}
             sums = {}
@@ -219,10 +173,57 @@ def tile_decodertreernn_pa_kernel(
                             identity[:],
                         )
 
+            def bring_states():
+                x_words = x_raw[:].bitcast(F32)
+                x_flipped = flip_psum.tile([P, BANK], F32, name="flipped")
+                for w in range(WORD_BLOCKS):
+                    nc.tensor.transpose(
+                        x_flipped[:, w * P : (w + 1) * P], x_words[:, every_second_word(w)], identity[:]
+                    )
+                nc.vector.tensor_copy(
+                    out=x_grouped[:].rearrange("p (g j u) -> p g j u", g=PASSES, u=PAIR),
+                    in_=x_flipped[:].rearrange("p (g u j) -> p g j u", g=PASSES, u=PAIR),
+                )
+
+            def quantise_states():
+                for g in range(PASSES):
+                    nc.vector.quantize_mx(
+                        out=x_codes[g][:].bitcast(FP8X4),
+                        scales=x_scales[g][:],
+                        in_=x_grouped[:, g * BLOCK : (g + 1) * BLOCK].bitcast(BF16),
+                    )
+
+            def state_values(blk):
+                g, u = divmod(blk, PAIR)
+                values = x_grouped[:].bitcast(BF16)[:, g * PAIR * BLOCK : (g + 1) * PAIR * BLOCK]
+                return values.rearrange("p (j u e) -> p u e j", u=PAIR, e=PAIR)[:, u]
+
+            def transpose_biases():
+                b_flipped = flip_psum.tile([P, BANK], F32, name="flipped")
+                bias_words = bias_raw[:].bitcast(F32)
+                for u in range(PAIR):
+                    nc.tensor.transpose(
+                        b_flipped[:, u * P : (u + 1) * P], bias_words[:, every_second_word(u)], identity[:]
+                    )
+                return b_flipped
+
+            def spread_biases(b_flipped):
+                nc.vector.tensor_copy(
+                    out=bias[:].rearrange("p (r u e) -> p r u e", u=PAIR, e=PAIR),
+                    in_=b_flipped[:, 0 : PAIR * P].bitcast(BF16).rearrange(
+                        "p (u r e) -> p r u e", u=PAIR, e=PAIR
+                    )[:, 0 : SIDES * 2 * rows],
+                )
+                by_kind = bias[:].rearrange("p (s kind c) -> p s kind c", s=SIDES, kind=2)
+                rz_cols = 2 * BLOCKS * PAIR
+                nc.vector.tensor_add(
+                    out=bias_rz[:], in0=by_kind[:, :, 0, 0:rz_cols], in1=by_kind[:, :, 1, 0:rz_cols]
+                )
+
             def empty_bank(n, e):
                 if e == 0:
                     grouped[n] = stage.tile([P, PAIR * BANK], F32, align_bytes=64, name="grouped")
-                by_vector = n % GATES == GATES - 1 and e == PAIR - 1
+                by_vector = e == PAIR - 1 and n % (2 * GROUP_PAIRS) in (3, 5)
                 copy = nc.vector.tensor_copy if by_vector else nc.scalar.copy
                 copy(
                     out=grouped[n][:, e * BANK : (e + 1) * BANK].rearrange(
@@ -242,72 +243,129 @@ def tile_decodertreernn_pa_kernel(
                 sums[n] = gates1.tile([P, PAIR, ROOTS], F32, name="sums")
                 multiply(sums[n], n, x_codes, x_scales)
 
-            def activate(n, e):
-                m = n - MULTIPLY_LAG
-                if n % GATES == GATES - 1:
-                    m = n - TANH_LAG
-                if not 0 <= m < SLABS:
-                    return
-                blk, side, gate = slabs[m]
-                i = m // GATES
-                if gate == GATES - 1:
-                    tanh(cand[i], side, blk, e)
-                    return
-                gate_out = (reset, update)[gate]
-                if e == 0:
-                    gate_out[i] = work1.tile([P, PAIR, ROOTS], F32, name=("reset", "update")[gate])
-                sigmoid(gate_out[i], sums[m], side, gate, blk, e)
-
-            def vector_share(n, half):
-                turn = n % GATES
-                m = n - (MIX_LAG, CAST_LAG, MULTIPLY_LAG)[turn]
-                if 0 <= m < SLABS:
-                    blk, side, gate = slabs[m]
-                    i = m // GATES
-                    nodes = slice(side * ROOTS, (side + 1) * ROOTS)
-                    g, u = divmod(blk, PAIR)
-                    if turn == 2:
-                        if half == 0:
-                            cand[i] = work1.tile([P, PAIR, ROOTS], F32, name="cand")
-                        reset_candidate(cand[i], sums[m], reset[i], side, blk, half)
-                    elif turn == 0 and half == 0:
-                        diff[i] = work1.tile([P, PAIR, ROOTS], F32, name="diff")
-                        nc.vector.tensor_sub(out=diff[i][:], in0=x_f32[:, blk, :, :], in1=cand[i][:])
-                    elif turn == 0:
-                        nc.vector.tensor_mul(out=diff[i][:], in0=update[i][:], in1=diff[i][:])
-                    elif half == 0:
-                        nc.vector.tensor_add(
-                            out=c_f32[blk][:, :, nodes], in0=diff[i][:], in1=cand[i][:]
-                        )
-                    else:
-                        nc.vector.tensor_copy(
-                            out=c_grouped[g][:, nodes, u * PAIR : (u + 1) * PAIR],
-                            in_=c_f32[blk][:, :, nodes].rearrange("p e j -> p j e"),
-                        )
-                m = n - QUANTISE_LAG
-                if turn == 2 and half == 1 and 0 <= m < SLABS:
-                    blk, side, gate = slabs[m]
-                    g, u = divmod(blk, PAIR)
-                    if u == PAIR - 1 and side == SIDES - 1:
-                        nc.vector.quantize_mx(
-                            out=c_codes[g][:].bitcast(FP8X4),
-                            scales=c_scales[g][:],
-                            in_=c_grouped[g][:].rearrange("p c t -> p (c t)"),
-                        )
-
-            for n in range(SLABS + QUANTISE_LAG + 1):
-                if n < SLABS:
-                    transpose_slab(n)
-                if 0 <= n - MULTIPLY_LAG < SLABS:
-                    multiply_slab(n - MULTIPLY_LAG)
-                vector_share(n, 0)
-                if 0 <= n - 1 < SLABS:
-                    quantise_slab(n - 1)
-                vector_share(n, 1)
+            def gate_on(gates, name, blk, side, gate):
+                gates[(blk, side)] = work1.tile([P, PAIR, ROOTS], F32, name="%s%d" % (name, side))
                 for e in range(PAIR):
-                    if n < SLABS:
-                        empty_bank(n, e)
-                    activate(n, e)
+                    sigmoid(gates[(blk, side)], sums[slab_of[(blk, side, gate)]], side, gate, blk, e)
+
+            def reset_on(blk, side):
+                gate_on(reset, "reset", blk, side, 0)
+
+            def update_on(blk, side):
+                gate_on(update, "update", blk, side, 1)
+
+            def candidate(blk, side):
+                cand[(blk, side)] = work1.tile([P, PAIR, ROOTS], F32, name="cand%d" % side)
+                for e in range(PAIR):
+                    reset_candidate(
+                        cand[(blk, side)], sums[slab_of[(blk, side, 2)]], reset[(blk, side)], side, blk, e
+                    )
+
+            def candidate_on(blk, side):
+                for e in range(PAIR):
+                    tanh(cand[(blk, side)], side, blk, e)
+
+            def mix_sub(blk, side):
+                diff[(blk, side)] = work1.tile([P, PAIR, ROOTS], F32, name="diff%d" % side)
+                nc.vector.tensor_sub(
+                    out=diff[(blk, side)][:], in0=state_values(blk), in1=cand[(blk, side)][:]
+                )
+
+            def mix_mul(blk, side):
+                both = diff[(blk, side)][:]
+                nc.vector.tensor_mul(out=both, in0=update[(blk, side)][:], in1=both)
+
+            def nodes_of(side):
+                return slice(side * ROOTS, (side + 1) * ROOTS)
+
+            def mix_add(blk, side):
+                g, u = divmod(blk, PAIR)
+                nc.vector.tensor_add(
+                    out=c_f32[g][:, u, :, nodes_of(side)],
+                    in0=diff[(blk, side)][:],
+                    in1=cand[(blk, side)][:],
+                )
+
+            def round_states(g, side):
+                nc.vector.tensor_copy(
+                    out=c_grouped[g][:, nodes_of(side), :].rearrange("p j (u e) -> p j u e", u=PAIR),
+                    in_=c_f32[g][:, :, :, nodes_of(side)].rearrange("p u e j -> p j u e"),
+                )
+
+            def quantise_children(g):
+                nc.vector.quantize_mx(
+                    out=c_codes[g][:].bitcast(FP8X4),
+                    scales=c_scales[g][:],
+                    in_=c_grouped[g][:].rearrange("p c t -> p (c t)"),
+                )
+
+            for i in range(PAIRS + GROUP_PAIRS + 2):
+                if i < PAIRS:
+                    transpose_slab(2 * i)
+                    if i == 0:
+                        bring_states()
+                    transpose_slab(2 * i + 1)
+                if 1 <= i <= PAIRS:
+                    quantise_slab(2 * i - 1)
+                if i == 2:
+                    spread_biases(b_flipped)
+
+                q, turn = divmod(i - 2, GROUP_PAIRS)
+                now = 0 <= q < BLOCKS
+                late = 0 <= q - 1 < BLOCKS
+                full = late and (q - 1) % PAIR == PAIR - 1
+                g = (q - 1) // PAIR
+                if turn == 0:
+                    if late:
+                        update_on(q - 1, 1)
+                    if now:
+                        reset_on(q, 0)
+                elif turn == 1 and now:
+                    reset_on(q, 1)
+                elif turn == 2 and now:
+                    update_on(q, 0)
+                if 1 <= i <= PAIRS:
+                    multiply_slab(2 * i - 2)
+                    multiply_slab(2 * i - 1)
+                if i == 1:
+                    b_flipped = transpose_biases()
+                if i < PAIRS:
+                    empty_bank(2 * i, 0)
+                    empty_bank(2 * i, 1)
+                if turn == 0:
+                    if late:
+                        mix_mul(q - 1, 1)
+                    if now:
+                        candidate(q, 0)
+                    if late:
+                        mix_add(q - 1, 0)
+                elif turn == 1:
+                    if now:
+                        candidate_on(q, 0)
+                        candidate(q, 1)
+                    if full:
+                        round_states(g, 0)
+                elif now:
+                    candidate_on(q, 1)
+                    mix_mul(q, 0)
+                if i == 0:
+                    quantise_states()
+                if i < PAIRS:
+                    quantise_slab(2 * i)
+                    empty_bank(2 * i + 1, 0)
+                    empty_bank(2 * i + 1, 1)
+                if turn == 0 and late:
+                    mix_add(q - 1, 1)
+                elif turn == 1:
+                    if now:
+                        mix_sub(q, 0)
+                    if full:
+                        round_states(g, 1)
+                elif turn == 2:
+                    if now:
+                        mix_sub(q, 1)
+                    if full:
+                        quantise_children(g)
 
         with tc.tile_pool(name="work2", bufs=5) as work2, tc.psum_pool(
             name="gates2", bufs=2
@@ -318,11 +376,10 @@ def tile_decodertreernn_pa_kernel(
 
             def gates_of_block(k):
                 side2, blk = blocks2[k]
-                banks = []
-                for gate in range(GATES):
-                    bank = gates2.tile([P, PAIR, children], F32, name="sums%d" % gate)
-                    multiply(bank, slab_index(blk, side2, gate), c_codes, c_scales)
-                    banks.append(bank)
+                banks = {}
+                for gate in (0, 2, 1):
+                    banks[gate] = gates2.tile([P, PAIR, children], F32, name="sums%d" % gate)
+                    multiply(banks[gate], slab_of[(blk, side2, gate)], c_codes, c_scales)
                 return banks
 
             def activate_block(k, banks):
@@ -332,32 +389,30 @@ def tile_decodertreernn_pa_kernel(
                 cand2[k] = work2.tile([P, PAIR, children], F32, name="cand2")
                 for e in range(PAIR):
                     sigmoid(reset2, banks[0], side2, 0, blk, e)
-                if k >= 1:
-                    mix_begin(k - 1)
                 for e in range(PAIR):
+                    if k >= 1:
+                        (mix_sub2, mix_mul2)[e](k - 1)
                     reset_candidate(cand2[k], banks[2], reset2, side2, blk, e)
+                if k >= 1:
+                    mix_add2(k - 1)
                 for e in range(PAIR):
                     sigmoid(update2[k], banks[1], side2, 1, blk, e)
+                if k >= 3:
+                    store_piece(k - 3)
                 for e in range(PAIR):
                     tanh(cand2[k], side2, blk, e)
 
-            def mix_begin(k):
+            def mix_sub2(k):
                 side2, blk = blocks2[k]
                 mixed[k] = work2.tile([P, PAIR, children], F32, name="mixed")
-                for e in range(PAIR):
-                    nc.vector.tensor_sub(
-                        out=mixed[k][:, e, :], in0=c_f32[blk][:, e, :], in1=cand2[k][:, e, :]
-                    )
+                g, u = divmod(blk, PAIR)
+                nc.vector.tensor_sub(out=mixed[k][:], in0=c_f32[g][:, u], in1=cand2[k][:])
 
-            def mix_end(k):
-                for e in range(PAIR):
-                    nc.vector.tensor_mul(
-                        out=mixed[k][:, e, :], in0=update2[k][:, e, :], in1=mixed[k][:, e, :]
-                    )
-                for e in range(PAIR):
-                    nc.vector.tensor_add(
-                        out=mixed[k][:, e, :], in0=mixed[k][:, e, :], in1=cand2[k][:, e, :]
-                    )
+            def mix_mul2(k):
+                nc.vector.tensor_mul(out=mixed[k][:], in0=update2[k][:], in1=mixed[k][:])
+
+            def mix_add2(k):
+                nc.vector.tensor_add(out=mixed[k][:], in0=mixed[k][:], in1=cand2[k][:])
 
             def transpose_back(i):
                 m, s = divmod(i, SIDES)
@@ -389,9 +444,9 @@ def tile_decodertreernn_pa_kernel(
                     transpose_back(k - 3)
                 if k < count:
                     activate_block(k, banks)
-                elif k == count:
-                    mix_begin(k - 1)
-                if 1 <= k <= count:
-                    mix_end(k - 1)
-                if k >= 3:
+                else:
+                    if k == count:
+                        mix_sub2(k - 1)
+                        mix_mul2(k - 1)
+                        mix_add2(k - 1)
                     store_piece(k - 3)

@@ -223,7 +223,7 @@ def tile_decodertreernn_pa_kernel(
             def empty_bank(n, e):
                 if e == 0:
                     grouped[n] = stage.tile([P, PAIR * BANK], F32, align_bytes=64, name="grouped")
-                by_vector = e == PAIR - 1 and n % (2 * GROUP_PAIRS) in (3, 5)
+                by_vector = (n % (2 * GROUP_PAIRS), e) in ((3, 1), (4, 0))
                 copy = nc.vector.tensor_copy if by_vector else nc.scalar.copy
                 copy(
                     out=grouped[n][:, e * BANK : (e + 1) * BANK].rearrange(
@@ -232,21 +232,31 @@ def tile_decodertreernn_pa_kernel(
                     in_=flipped[(n, e)][:].rearrange("p (g u q) -> p g q u", g=PASSES, u=PAIR),
                 )
 
-            def quantise_slab(n):
+            def quantise_rows(n, parities):
+                cols = slice(parities[0] * BLOCK, (parities[-1] + 1) * BLOCK)
+                words = slice(parities[0] * BANK, (parities[-1] + 1) * BANK)
                 nc.vector.quantize_mx(
-                    out=w_codes[n][:].bitcast(FP8X4),
-                    scales=w_scales[n][:],
-                    in_=grouped[n][:].bitcast(BF16),
+                    out=w_codes[n][:, cols].bitcast(FP8X4),
+                    scales=w_scales[n][:, cols],
+                    in_=grouped[n][:, words].bitcast(BF16),
                 )
+
+            def quantise_slab(n):
+                quantise_rows(n, range(PAIR))
 
             def multiply_slab(n):
                 sums[n] = gates1.tile([P, PAIR, ROOTS], F32, name="sums")
                 multiply(sums[n], n, x_codes, x_scales)
 
+            def sides_tile(tiles, name, blk):
+                if blk not in tiles:
+                    tiles[blk] = work1.tile([P, SIDES, PAIR, ROOTS], F32, name=name)
+                return tiles[blk]
+
             def gate_on(gates, name, blk, side, gate):
-                gates[(blk, side)] = work1.tile([P, PAIR, ROOTS], F32, name="%s%d" % (name, side))
+                gate_out = sides_tile(gates, name, blk)[:, side]
                 for e in range(PAIR):
-                    sigmoid(gates[(blk, side)], sums[slab_of[(blk, side, gate)]], side, gate, blk, e)
+                    sigmoid(gate_out, sums[slab_of[(blk, side, gate)]], side, gate, blk, e)
 
             def reset_on(blk, side):
                 gate_on(reset, "reset", blk, side, 0)
@@ -255,117 +265,156 @@ def tile_decodertreernn_pa_kernel(
                 gate_on(update, "update", blk, side, 1)
 
             def candidate(blk, side):
-                cand[(blk, side)] = work1.tile([P, PAIR, ROOTS], F32, name="cand%d" % side)
+                cand_out = sides_tile(cand, "cand", blk)[:, side]
                 for e in range(PAIR):
                     reset_candidate(
-                        cand[(blk, side)], sums[slab_of[(blk, side, 2)]], reset[(blk, side)], side, blk, e
+                        cand_out, sums[slab_of[(blk, side, 2)]], reset[blk][:, side], side, blk, e
                     )
 
             def candidate_on(blk, side):
                 for e in range(PAIR):
-                    tanh(cand[(blk, side)], side, blk, e)
+                    tanh(cand[blk][:, side], side, blk, e)
 
             def mix_sub(blk, side):
-                diff[(blk, side)] = work1.tile([P, PAIR, ROOTS], F32, name="diff%d" % side)
                 nc.vector.tensor_sub(
-                    out=diff[(blk, side)][:], in0=state_values(blk), in1=cand[(blk, side)][:]
+                    out=sides_tile(diff, "diff", blk)[:, side],
+                    in0=state_values(blk),
+                    in1=cand[blk][:, side],
                 )
 
-            def mix_mul(blk, side):
-                both = diff[(blk, side)][:]
-                nc.vector.tensor_mul(out=both, in0=update[(blk, side)][:], in1=both)
+            both = slice(0, SIDES)
+
+            def mix_mul(blk, sides):
+                nc.vector.tensor_mul(
+                    out=diff[blk][:, sides], in0=update[blk][:, sides], in1=diff[blk][:, sides]
+                )
 
             def nodes_of(side):
                 return slice(side * ROOTS, (side + 1) * ROOTS)
 
-            def mix_add(blk, side):
+            def mix_add(blk):
                 g, u = divmod(blk, PAIR)
                 nc.vector.tensor_add(
-                    out=c_f32[g][:, u, :, nodes_of(side)],
-                    in0=diff[(blk, side)][:],
-                    in1=cand[(blk, side)][:],
+                    out=c_f32[g][:, u].rearrange("p e (s j) -> p s e j", s=SIDES),
+                    in0=diff[blk][:],
+                    in1=cand[blk][:],
                 )
 
-            def round_states(g, side):
+            def round_states(g):
                 nc.vector.tensor_copy(
-                    out=c_grouped[g][:, nodes_of(side), :].rearrange("p j (u e) -> p j u e", u=PAIR),
-                    in_=c_f32[g][:, :, :, nodes_of(side)].rearrange("p u e j -> p j u e"),
+                    out=c_grouped[g][:].rearrange("p j (u e) -> p j u e", u=PAIR),
+                    in_=c_f32[g][:].rearrange("p u e j -> p j u e"),
                 )
 
-            def quantise_children(g):
+            def mix_round(blk, side):
+                g, u = divmod(blk, PAIR)
+                nc.vector.tensor_add(
+                    out=c_grouped[g][:, nodes_of(side), u * PAIR : (u + 1) * PAIR],
+                    in0=diff[blk][:, side].rearrange("p e j -> p j e"),
+                    in1=cand[blk][:, side].rearrange("p e j -> p j e"),
+                )
+
+            def quantise_children(g, side):
                 nc.vector.quantize_mx(
-                    out=c_codes[g][:].bitcast(FP8X4),
-                    scales=c_scales[g][:],
-                    in_=c_grouped[g][:].rearrange("p c t -> p (c t)"),
+                    out=c_codes[g][:, nodes_of(side)].bitcast(FP8X4),
+                    scales=c_scales[g][:, nodes_of(side)],
+                    in_=c_grouped[g][:, nodes_of(side), :].rearrange("p c t -> p (c t)"),
                 )
 
-            for i in range(PAIRS + GROUP_PAIRS + 2):
-                if i < PAIRS:
-                    transpose_slab(2 * i)
-                    if i == 0:
-                        bring_states()
-                    transpose_slab(2 * i + 1)
-                if 1 <= i <= PAIRS:
+            last = PAIRS - 1
+            for i in range(last):
+                transpose_slab(2 * i)
+                if i == 0:
+                    bring_states()
+                transpose_slab(2 * i + 1)
+                if i >= 1:
                     quantise_slab(2 * i - 1)
                 if i == 2:
                     spread_biases(b_flipped)
 
                 q, turn = divmod(i - 2, GROUP_PAIRS)
-                now = 0 <= q < BLOCKS
-                late = 0 <= q - 1 < BLOCKS
-                full = late and (q - 1) % PAIR == PAIR - 1
-                g = (q - 1) // PAIR
+                now = q >= 0
+                late = q >= 1
                 if turn == 0:
                     if late:
                         update_on(q - 1, 1)
-                    if now:
-                        reset_on(q, 0)
+                    reset_on(q, 0)
                 elif turn == 1 and now:
                     reset_on(q, 1)
                 elif turn == 2 and now:
                     update_on(q, 0)
-                if 1 <= i <= PAIRS:
+                if i >= 1:
                     multiply_slab(2 * i - 2)
                     multiply_slab(2 * i - 1)
                 if i == 1:
                     b_flipped = transpose_biases()
-                if i < PAIRS:
-                    empty_bank(2 * i, 0)
-                    empty_bank(2 * i, 1)
+                empty_bank(2 * i, 0)
+                empty_bank(2 * i, 1)
                 if turn == 0:
                     if late:
-                        mix_mul(q - 1, 1)
-                    if now:
-                        candidate(q, 0)
-                    if late:
-                        mix_add(q - 1, 0)
-                elif turn == 1:
-                    if now:
-                        candidate_on(q, 0)
-                        candidate(q, 1)
-                    if full:
-                        round_states(g, 0)
-                elif now:
+                        mix_mul(q - 1, both)
+                    candidate(q, 0)
+                elif turn == 1 and now:
+                    candidate_on(q, 0)
+                    candidate(q, 1)
+                    if q == PAIR:
+                        round_states(0)
+                elif turn == 2 and now:
                     candidate_on(q, 1)
-                    mix_mul(q, 0)
+                    if q == PAIR:
+                        for side in range(SIDES):
+                            quantise_children(0, side)
                 if i == 0:
                     quantise_states()
-                if i < PAIRS:
-                    quantise_slab(2 * i)
-                    empty_bank(2 * i + 1, 0)
-                    empty_bank(2 * i + 1, 1)
+                quantise_slab(2 * i)
+                empty_bank(2 * i + 1, 0)
+                empty_bank(2 * i + 1, 1)
                 if turn == 0 and late:
-                    mix_add(q - 1, 1)
-                elif turn == 1:
-                    if now:
-                        mix_sub(q, 0)
-                    if full:
-                        round_states(g, 1)
-                elif turn == 2:
-                    if now:
-                        mix_sub(q, 1)
-                    if full:
-                        quantise_children(g)
+                    mix_add(q - 1)
+                elif turn == 1 and now:
+                    mix_sub(q, 0)
+                elif turn == 2 and now:
+                    mix_sub(q, 1)
+
+            blk = BLOCKS - 1
+            g = blk // PAIR
+            left, right = 2 * last, 2 * last + 1
+            transpose_slab(left)
+            quantise_slab(left - 1)
+            update_on(blk - 1, 1)
+            reset_on(blk, 0)
+            multiply_slab(left - 2)
+            multiply_slab(left - 1)
+            transpose_slab(right)
+            mix_mul(blk - 1, both)
+            candidate(blk, 0)
+            empty_bank(left, 0)
+            empty_bank(left, 1)
+            mix_round(blk - 1, 0)
+            candidate_on(blk, 0)
+            reset_on(blk, 1)
+            quantise_slab(left)
+            multiply_slab(left)
+            candidate(blk, 1)
+            mix_sub(blk, 0)
+            empty_bank(right, 0)
+            candidate_on(blk, 1)
+            empty_bank(right, 1)
+            update_on(blk, 0)
+            mix_round(blk - 1, 1)
+            quantise_rows(right, [0])
+            mix_sub(blk, 1)
+            quantise_rows(right, [1])
+            multiply_slab(right)
+            mix_mul(blk, slice(0, 1))
+            update_on(blk, 1)
+            mix_add(blk - 1)
+            mix_round(blk, 0)
+            mix_mul(blk, slice(1, SIDES))
+            quantise_children(g, 0)
+            mix_round(blk, 1)
+            mix_add(blk)
+            quantise_children(g, 1)
 
         with tc.tile_pool(name="work2", bufs=5) as work2, tc.psum_pool(
             name="gates2", bufs=2
@@ -387,29 +436,53 @@ def tile_decodertreernn_pa_kernel(
                 reset2 = work2.tile([P, PAIR, children], F32)
                 update2[k] = work2.tile([P, PAIR, children], F32, name="update2")
                 cand2[k] = work2.tile([P, PAIR, children], F32, name="cand2")
+                def update_on2(e):
+                    sigmoid(update2[k], banks[1], side2, 1, blk, e)
+
+                leaves = k >= 3 and not leaves_by_vector(k - 3)
                 for e in range(PAIR):
                     sigmoid(reset2, banks[0], side2, 0, blk, e)
-                for e in range(PAIR):
-                    if k >= 1:
-                        (mix_sub2, mix_mul2)[e](k - 1)
-                    reset_candidate(cand2[k], banks[2], reset2, side2, blk, e)
                 if k >= 1:
-                    mix_add2(k - 1)
-                for e in range(PAIR):
-                    sigmoid(update2[k], banks[1], side2, 1, blk, e)
-                if k >= 3:
+                    mix_sub2(k - 1)
+                reset_candidate(cand2[k], banks[2], reset2, side2, blk, 0)
+                if k >= 1 and not added_by_tensor(k - 1):
+                    mix_mul2(k - 1)
+                reset_candidate(cand2[k], banks[2], reset2, side2, blk, 1)
+                if k >= 1:
+                    if added_by_tensor(k - 1):
+                        mix_mul2(k - 1)
+                    else:
+                        mix_add2(k - 1)
+                if leaves:
                     store_piece(k - 3)
+                else:
+                    update_on2(0)
                 for e in range(PAIR):
                     tanh(cand2[k], side2, blk, e)
+                for e in range(0 if leaves else 1, PAIR):
+                    update_on2(e)
+                if k >= 3 and not leaves:
+                    store_piece(k - 3)
 
-            def mix_sub2(k):
+            def added_by_tensor(k):
+                return k // PAIR % 2 == 1
+
+            def leaves_by_vector(i):
+                return i % 4 == 0 or i == len(blocks2) - 1
+
+            def mix_sub2(k, nodes=slice(0, SIDES * ROOTS)):
                 side2, blk = blocks2[k]
-                mixed[k] = work2.tile([P, PAIR, children], F32, name="mixed")
+                if nodes.start == 0:
+                    mixed[k] = work2.tile([P, PAIR, children], F32, name="mixed")
                 g, u = divmod(blk, PAIR)
-                nc.vector.tensor_sub(out=mixed[k][:], in0=c_f32[g][:, u], in1=cand2[k][:])
+                nc.vector.tensor_sub(
+                    out=mixed[k][:, :, nodes], in0=c_f32[g][:, u, :, nodes], in1=cand2[k][:, :, nodes]
+                )
 
-            def mix_mul2(k):
-                nc.vector.tensor_mul(out=mixed[k][:], in0=update2[k][:], in1=mixed[k][:])
+            def mix_mul2(k, nodes=slice(0, SIDES * ROOTS)):
+                nc.vector.tensor_mul(
+                    out=mixed[k][:, :, nodes], in0=update2[k][:, :, nodes], in1=mixed[k][:, :, nodes]
+                )
 
             def mix_add2(k):
                 nc.vector.tensor_add(out=mixed[k][:], in0=mixed[k][:], in1=cand2[k][:])
@@ -418,19 +491,26 @@ def tile_decodertreernn_pa_kernel(
                 m, s = divmod(i, SIDES)
                 back[i] = back_psum.tile([P, PAIR, PAIR, P], F32, name="back")
                 for u in range(PAIR):
+                    k = m * PAIR + u
+                    terms = [cand2[k], mixed[k]] if added_by_tensor(k) else [mixed[k]]
                     for e in range(PAIR):
-                        nc.tensor.transpose(
-                            back[i][:, u, e, :],
-                            mixed[m * PAIR + u][:, e, s * ROOTS : (s + 1) * ROOTS],
-                            identity[:],
-                        )
+                        for t, term in enumerate(terms):
+                            nc.tensor.matmul(
+                                out=back[i][:, u, e, :],
+                                lhsT=term[:, e, s * ROOTS : (s + 1) * ROOTS],
+                                rhs=identity[:],
+                                start=(t == 0),
+                                stop=(t == len(terms) - 1),
+                                is_transpose=True,
+                            )
 
             def store_piece(i):
                 m, s = divmod(i, SIDES)
                 side2, g = divmod(m, PASSES)
                 cols = slice(g * PAIR * BLOCK, (g + 1) * PAIR * BLOCK)
                 leaving = work2.tile([P, PAIR * BLOCK], F32)
-                nc.scalar.copy(
+                copy = nc.vector.tensor_copy if leaves_by_vector(i) else nc.scalar.copy
+                copy(
                     out=leaving[:].rearrange("j (q u e) -> j q u e", u=PAIR, e=PAIR),
                     in_=back[i][:].rearrange("j u e q -> j q u e"),
                 )
@@ -446,7 +526,9 @@ def tile_decodertreernn_pa_kernel(
                     activate_block(k, banks)
                 else:
                     if k == count:
-                        mix_sub2(k - 1)
-                        mix_mul2(k - 1)
-                        mix_add2(k - 1)
+                        halves = [slice(s * ROOTS, (s + 1) * ROOTS) for s in range(SIDES)]
+                        for nodes in halves:
+                            mix_sub2(k - 1, nodes)
+                        for nodes in halves:
+                            mix_mul2(k - 1, nodes)
                     store_piece(k - 3)

@@ -326,7 +326,6 @@ def tile_decodertreernn_pa_kernel(
                 transpose_slab(2 * i)
                 if i == 0:
                     bring_states()
-                transpose_slab(2 * i + 1)
                 if i >= 1:
                     quantise_slab(2 * i - 1)
                 if i == 2:
@@ -345,6 +344,8 @@ def tile_decodertreernn_pa_kernel(
                     update_on(q, 0)
                 if i >= 1:
                     multiply_slab(2 * i - 2)
+                transpose_slab(2 * i + 1)
+                if i >= 1:
                     multiply_slab(2 * i - 1)
                 if i == 1:
                     b_flipped = transpose_biases()

@@ -199,20 +199,20 @@ def tile_decodertreernn_pa_kernel(
                 return values.rearrange("p (j u e) -> p u e j", u=PAIR, e=PAIR)[:, u]
 
             def transpose_biases():
-                b_flipped = flip_psum.tile([P, BANK], F32, name="flipped")
+                b_flipped = gates1.tile([P, PAIR, P], F32, name="sums")
                 bias_words = bias_raw[:].bitcast(F32)
                 for u in range(PAIR):
                     nc.tensor.transpose(
-                        b_flipped[:, u * P : (u + 1) * P], bias_words[:, every_second_word(u)], identity[:]
+                        b_flipped[:, u, :], bias_words[:, every_second_word(u)], identity[:]
                     )
                 return b_flipped
 
             def spread_biases(b_flipped):
                 nc.vector.tensor_copy(
                     out=bias[:].rearrange("p (r u e) -> p r u e", u=PAIR, e=PAIR),
-                    in_=b_flipped[:, 0 : PAIR * P].bitcast(BF16).rearrange(
-                        "p (u r e) -> p r u e", u=PAIR, e=PAIR
-                    )[:, 0 : SIDES * 2 * rows],
+                    in_=b_flipped[:].bitcast(BF16).rearrange("p u (r e) -> p r u e", e=PAIR)[
+                        :, 0 : SIDES * 2 * rows
+                    ],
                 )
                 by_kind = bias[:].rearrange("p (s kind c) -> p s kind c", s=SIDES, kind=2)
                 rz_cols = 2 * BLOCKS * PAIR
@@ -328,8 +328,8 @@ def tile_decodertreernn_pa_kernel(
                     bring_states()
                 if i >= 1:
                     quantise_slab(2 * i - 1)
-                if i == 2:
-                    spread_biases(b_flipped)
+                if i == 1:
+                    b_flipped = transpose_biases()
 
                 q, turn = divmod(i - 2, GROUP_PAIRS)
                 now = q >= 0
@@ -344,13 +344,11 @@ def tile_decodertreernn_pa_kernel(
                     update_on(q, 0)
                 if i >= 1:
                     multiply_slab(2 * i - 2)
+                empty_bank(2 * i, 0)
+                empty_bank(2 * i, 1)
                 transpose_slab(2 * i + 1)
                 if i >= 1:
                     multiply_slab(2 * i - 1)
-                if i == 1:
-                    b_flipped = transpose_biases()
-                empty_bank(2 * i, 0)
-                empty_bank(2 * i, 1)
                 if turn == 0:
                     if late:
                         mix_mul(q - 1, both)
@@ -376,6 +374,8 @@ def tile_decodertreernn_pa_kernel(
                     mix_sub(q, 0)
                 elif turn == 2 and now:
                     mix_sub(q, 1)
+                if i == 1:
+                    spread_biases(b_flipped)
 
             blk = BLOCKS - 1
             g = blk // PAIR
@@ -397,32 +397,34 @@ def tile_decodertreernn_pa_kernel(
             quantise_slab(left)
             multiply_slab(left)
             candidate(blk, 1)
-            mix_sub(blk, 0)
             empty_bank(right, 0)
-            candidate_on(blk, 1)
             empty_bank(right, 1)
-            update_on(blk, 0)
-            mix_round(blk - 1, 1)
             quantise_rows(right, [0])
-            mix_sub(blk, 1)
+            candidate_on(blk, 1)
+            mix_sub(blk, 0)
+            update_on(blk, 0)
             quantise_rows(right, [1])
             multiply_slab(right)
+            mix_round(blk - 1, 1)
+            mix_sub(blk, 1)
             mix_mul(blk, slice(0, 1))
             update_on(blk, 1)
-            mix_add(blk - 1)
             mix_round(blk, 0)
             mix_mul(blk, slice(1, SIDES))
             quantise_children(g, 0)
             mix_round(blk, 1)
-            mix_add(blk)
             quantise_children(g, 1)
+            mix_add(blk - 1)
+            mix_add(blk)
 
         with tc.tile_pool(name="work2", bufs=5) as work2, tc.psum_pool(
             name="gates2", bufs=2
         ) as gates2, tc.psum_pool(name="back", bufs=2) as back_psum:
             children = SIDES * ROOTS
             blocks2 = [(side2, blk) for side2 in range(SIDES) for blk in range(BLOCKS)]
+            count = len(blocks2)
             update2, cand2, mixed, back = {}, {}, {}, {}
+            leaving_in = {4: 0, 6: 1, 7: 2, 9: 3}
 
             def gates_of_block(k):
                 side2, blk = blocks2[k]
@@ -432,44 +434,8 @@ def tile_decodertreernn_pa_kernel(
                     multiply(banks[gate], slab_of[(blk, side2, gate)], c_codes, c_scales)
                 return banks
 
-            def activate_block(k, banks):
-                side2, blk = blocks2[k]
-                reset2 = work2.tile([P, PAIR, children], F32)
-                update2[k] = work2.tile([P, PAIR, children], F32, name="update2")
-                cand2[k] = work2.tile([P, PAIR, children], F32, name="cand2")
-                def update_on2(e):
-                    sigmoid(update2[k], banks[1], side2, 1, blk, e)
-
-                leaves = k >= 3 and not leaves_by_vector(k - 3)
-                for e in range(PAIR):
-                    sigmoid(reset2, banks[0], side2, 0, blk, e)
-                if k >= 1:
-                    mix_sub2(k - 1)
-                reset_candidate(cand2[k], banks[2], reset2, side2, blk, 0)
-                if k >= 1 and not added_by_tensor(k - 1):
-                    mix_mul2(k - 1)
-                reset_candidate(cand2[k], banks[2], reset2, side2, blk, 1)
-                if k >= 1:
-                    if added_by_tensor(k - 1):
-                        mix_mul2(k - 1)
-                    else:
-                        mix_add2(k - 1)
-                if leaves:
-                    store_piece(k - 3)
-                else:
-                    update_on2(0)
-                for e in range(PAIR):
-                    tanh(cand2[k], side2, blk, e)
-                for e in range(0 if leaves else 1, PAIR):
-                    update_on2(e)
-                if k >= 3 and not leaves:
-                    store_piece(k - 3)
-
             def added_by_tensor(k):
-                return k // PAIR % 2 == 1
-
-            def leaves_by_vector(i):
-                return i % 4 == 0 or i == len(blocks2) - 1
+                return k >= count // 2
 
             def mix_sub2(k, nodes=slice(0, SIDES * ROOTS)):
                 side2, blk = blocks2[k]
@@ -488,6 +454,26 @@ def tile_decodertreernn_pa_kernel(
             def mix_add2(k):
                 nc.vector.tensor_add(out=mixed[k][:], in0=mixed[k][:], in1=cand2[k][:])
 
+            def activate_block(k, banks):
+                side2, blk = blocks2[k]
+                reset2 = work2.tile([P, PAIR, children], F32)
+                update2[k] = work2.tile([P, PAIR, children], F32, name="update2")
+                cand2[k] = work2.tile([P, PAIR, children], F32, name="cand2")
+                for e in range(PAIR):
+                    sigmoid(reset2, banks[0], side2, 0, blk, e)
+                if k >= 1:
+                    mix_sub2(k - 1)
+                for e in range(PAIR):
+                    reset_candidate(cand2[k], banks[2], reset2, side2, blk, e)
+                for e in range(PAIR):
+                    sigmoid(update2[k], banks[1], side2, 1, blk, e)
+                if k >= 1:
+                    mix_mul2(k - 1)
+                if k >= 2 and not added_by_tensor(k - 2):
+                    mix_add2(k - 2)
+                for e in range(PAIR):
+                    tanh(cand2[k], side2, blk, e)
+
             def transpose_back(i):
                 m, s = divmod(i, SIDES)
                 back[i] = back_psum.tile([P, PAIR, PAIR, P], F32, name="back")
@@ -505,31 +491,32 @@ def tile_decodertreernn_pa_kernel(
                                 is_transpose=True,
                             )
 
-            def store_piece(i):
+            def store_piece(i, copy):
                 m, s = divmod(i, SIDES)
                 side2, g = divmod(m, PASSES)
                 cols = slice(g * PAIR * BLOCK, (g + 1) * PAIR * BLOCK)
                 leaving = work2.tile([P, PAIR * BLOCK], F32)
-                copy = nc.vector.tensor_copy if leaves_by_vector(i) else nc.scalar.copy
                 copy(
                     out=leaving[:].rearrange("j (q u e) -> j q u e", u=PAIR, e=PAIR),
                     in_=back[i][:].rearrange("j u e q -> j q u e"),
                 )
                 nc.sync.dma_start(out=out_rows[:, s, side2, cols], in_=leaving[:])
 
-            count = len(blocks2)
-            for k in range(count + 3):
+            for k in range(count + 2):
                 if k < count:
                     banks = gates_of_block(k)
-                if k >= 3:
-                    transpose_back(k - 3)
+                m = leaving_in.get(k)
+                if m is not None:
+                    for s in range(SIDES):
+                        transpose_back(m * SIDES + s)
                 if k < count:
                     activate_block(k, banks)
-                else:
-                    if k == count:
-                        halves = [slice(s * ROOTS, (s + 1) * ROOTS) for s in range(SIDES)]
-                        for nodes in halves:
-                            mix_sub2(k - 1, nodes)
-                        for nodes in halves:
-                            mix_mul2(k - 1, nodes)
-                    store_piece(k - 3)
+                elif k == count:
+                    halves = [slice(s * ROOTS, (s + 1) * ROOTS) for s in range(SIDES)]
+                    for nodes in halves:
+                        mix_sub2(k - 1, nodes)
+                    for nodes in halves:
+                        mix_mul2(k - 1, nodes)
+                if m is not None:
+                    store_piece(m * SIDES, nc.scalar.copy)
+                    store_piece(m * SIDES + 1, nc.scalar.copy if k == count - 1 else nc.vector.tensor_copy)

@@ -82,10 +82,11 @@ def tile_decodertreernn_pa_kernel(
         ]
         bias = keep.tile([P, SIDES * 2 * GATES * BLOCKS * PAIR], F32)
         bias_rz = keep.tile([P, SIDES, 2 * BLOCKS * PAIR], F32)
+        bias_neg = keep.tile([P, SIDES * 2 * GATES * BLOCKS * PAIR], F32)
 
-        def bias_column(side, kind, gate, blk, e):
+        def bias_column(side, kind, gate, blk, e, table=bias):
             col = ((side * 2 + kind) * GATES * BLOCKS + gate * BLOCKS + blk) * PAIR + e
-            return bias[:, col : col + 1]
+            return table[:, col : col + 1]
 
         def bias_rz_column(side, gate, blk, e):
             col = (gate * BLOCKS + blk) * PAIR + e
@@ -135,6 +136,9 @@ def tile_decodertreernn_pa_kernel(
             name="gates1", bufs=4
         ) as gates1:
             x_raw = once.tile([P, H], BF16)
+            bias_raw = once.tile([P, PAIR * BLOCK], BF16)
+            nc.vector.memset(bias_raw[:], 0.0)
+            rows = GATES * PASSES
             raw = []
             for n, (blk, side, gate) in enumerate(slabs):
                 raw_slab = raw_pool.tile([P, PAIR * H], BF16, name="raw_slab")
@@ -147,9 +151,6 @@ def tile_decodertreernn_pa_kernel(
             nc.vector.memset(warm[:], 0.0)
             nc.scalar.activation(out=warm[:], in_=warm[:], func=ACT.Sigmoid)
 
-            bias_raw = once.tile([P, PAIR * BLOCK], BF16)
-            nc.vector.memset(bias_raw[:], 0.0)
-            rows = GATES * PASSES
             for v, vec in enumerate((bih_l, bhh_l, bih_r, bhh_r)):
                 nc.scalar.dma_start(
                     out=bias_raw[v * rows : (v + 1) * rows, :],
@@ -216,6 +217,7 @@ def tile_decodertreernn_pa_kernel(
                 )
                 by_kind = bias[:].rearrange("p (s kind c) -> p s kind c", s=SIDES, kind=2)
                 rz_cols = 2 * BLOCKS * PAIR
+                nc.vector.tensor_scalar_mul(bias_neg[:], bias[:], -1.0)
                 nc.vector.tensor_add(
                     out=bias_rz[:], in0=by_kind[:, :, 0, 0:rz_cols], in1=by_kind[:, :, 1, 0:rz_cols]
                 )
@@ -223,7 +225,7 @@ def tile_decodertreernn_pa_kernel(
             def empty_bank(n, e):
                 if e == 0:
                     grouped[n] = stage.tile([P, PAIR * BANK], F32, align_bytes=64, name="grouped")
-                by_vector = (n % (2 * GROUP_PAIRS), e) in ((3, 1), (4, 0))
+                by_vector = (n % (2 * GROUP_PAIRS), e) in ((3, 1), (4, 0)) and n < SLABS - 4
                 copy = nc.vector.tensor_copy if by_vector else nc.scalar.copy
                 copy(
                     out=grouped[n][:, e * BANK : (e + 1) * BANK].rearrange(
@@ -275,11 +277,11 @@ def tile_decodertreernn_pa_kernel(
                 for e in range(PAIR):
                     tanh(cand[blk][:, side], side, blk, e)
 
-            def mix_sub(blk, side):
+            def mix_sub(blk):
                 nc.vector.tensor_sub(
-                    out=sides_tile(diff, "diff", blk)[:, side],
-                    in0=state_values(blk),
-                    in1=cand[blk][:, side],
+                    out=sides_tile(diff, "diff", blk)[:],
+                    in0=state_values(blk).unsqueeze(1).to_broadcast([P, SIDES, PAIR, ROOTS]),
+                    in1=cand[blk][:],
                 )
 
             both = slice(0, SIDES)
@@ -328,9 +330,6 @@ def tile_decodertreernn_pa_kernel(
                     bring_states()
                 if i >= 1:
                     quantise_slab(2 * i - 1)
-                if i == 1:
-                    b_flipped = transpose_biases()
-
                 q, turn = divmod(i - 2, GROUP_PAIRS)
                 now = q >= 0
                 late = q >= 1
@@ -347,6 +346,8 @@ def tile_decodertreernn_pa_kernel(
                 empty_bank(2 * i, 0)
                 empty_bank(2 * i, 1)
                 transpose_slab(2 * i + 1)
+                if i == 1:
+                    b_flipped = transpose_biases()
                 if i >= 1:
                     multiply_slab(2 * i - 1)
                 if turn == 0:
@@ -357,12 +358,10 @@ def tile_decodertreernn_pa_kernel(
                     candidate_on(q, 0)
                     candidate(q, 1)
                     if q == PAIR:
-                        round_states(0)
-                elif turn == 2 and now:
-                    candidate_on(q, 1)
-                    if q == PAIR:
                         for side in range(SIDES):
                             quantise_children(0, side)
+                elif turn == 2 and now:
+                    candidate_on(q, 1)
                 if i == 0:
                     quantise_states()
                 quantise_slab(2 * i)
@@ -370,10 +369,10 @@ def tile_decodertreernn_pa_kernel(
                 empty_bank(2 * i + 1, 1)
                 if turn == 0 and late:
                     mix_add(q - 1)
-                elif turn == 1 and now:
-                    mix_sub(q, 0)
+                    if q == PAIR:
+                        round_states(0)
                 elif turn == 2 and now:
-                    mix_sub(q, 1)
+                    mix_sub(q)
                 if i == 1:
                     spread_biases(b_flipped)
 
@@ -391,7 +390,8 @@ def tile_decodertreernn_pa_kernel(
             candidate(blk, 0)
             empty_bank(left, 0)
             empty_bank(left, 1)
-            mix_round(blk - 1, 0)
+            for side in range(SIDES):
+                mix_round(blk - 1, side)
             candidate_on(blk, 0)
             reset_on(blk, 1)
             quantise_slab(left)
@@ -399,14 +399,12 @@ def tile_decodertreernn_pa_kernel(
             candidate(blk, 1)
             empty_bank(right, 0)
             empty_bank(right, 1)
-            quantise_rows(right, [0])
             candidate_on(blk, 1)
-            mix_sub(blk, 0)
+            quantise_rows(right, [0])
             update_on(blk, 0)
             quantise_rows(right, [1])
             multiply_slab(right)
-            mix_round(blk - 1, 1)
-            mix_sub(blk, 1)
+            mix_sub(blk)
             mix_mul(blk, slice(0, 1))
             update_on(blk, 1)
             mix_round(blk, 0)
@@ -423,8 +421,8 @@ def tile_decodertreernn_pa_kernel(
             children = SIDES * ROOTS
             blocks2 = [(side2, blk) for side2 in range(SIDES) for blk in range(BLOCKS)]
             count = len(blocks2)
-            update2, cand2, mixed, back = {}, {}, {}, {}
-            leaving_in = {4: 0, 6: 1, 7: 2, 9: 3}
+            update2, cand2, kept, back = {}, {}, {}, {}
+            leaving_in = {3: 0, 5: 1, 7: 2, 8: 3}
 
             def gates_of_block(k):
                 side2, blk = blocks2[k]
@@ -434,25 +432,23 @@ def tile_decodertreernn_pa_kernel(
                     multiply(banks[gate], slab_of[(blk, side2, gate)], c_codes, c_scales)
                 return banks
 
+            def carried(k):
+                g, u = divmod(blocks2[k][1], PAIR)
+                kept[k] = work2.tile([P, PAIR, children], F32, name="kept")
+                nc.vector.tensor_mul(out=kept[k][:], in0=update2[k][:], in1=c_f32[g][:, u])
+
+            def renewed(k, parities=slice(0, PAIR)):
+                part = cand2[k][:, parities]
+                nc.vector.scalar_tensor_tensor(
+                    out=part, in0=update2[k][:, parities], scalar=1.0, in1=part,
+                    op0=ALU.subtract, op1=ALU.mult,
+                )
+
             def added_by_tensor(k):
                 return k >= count // 2
 
-            def mix_sub2(k, nodes=slice(0, SIDES * ROOTS)):
-                side2, blk = blocks2[k]
-                if nodes.start == 0:
-                    mixed[k] = work2.tile([P, PAIR, children], F32, name="mixed")
-                g, u = divmod(blk, PAIR)
-                nc.vector.tensor_sub(
-                    out=mixed[k][:, :, nodes], in0=c_f32[g][:, u, :, nodes], in1=cand2[k][:, :, nodes]
-                )
-
-            def mix_mul2(k, nodes=slice(0, SIDES * ROOTS)):
-                nc.vector.tensor_mul(
-                    out=mixed[k][:, :, nodes], in0=update2[k][:, :, nodes], in1=mixed[k][:, :, nodes]
-                )
-
-            def mix_add2(k):
-                nc.vector.tensor_add(out=mixed[k][:], in0=mixed[k][:], in1=cand2[k][:])
+            def add_up(k):
+                nc.vector.tensor_add(out=kept[k][:], in0=kept[k][:], in1=cand2[k][:])
 
             def activate_block(k, banks):
                 side2, blk = blocks2[k]
@@ -462,28 +458,33 @@ def tile_decodertreernn_pa_kernel(
                 for e in range(PAIR):
                     sigmoid(reset2, banks[0], side2, 0, blk, e)
                 if k >= 1:
-                    mix_sub2(k - 1)
+                    renewed(k - 1)
                 for e in range(PAIR):
                     reset_candidate(cand2[k], banks[2], reset2, side2, blk, e)
                 for e in range(PAIR):
                     sigmoid(update2[k], banks[1], side2, 1, blk, e)
-                if k >= 1:
-                    mix_mul2(k - 1)
-                if k >= 2 and not added_by_tensor(k - 2):
-                    mix_add2(k - 2)
+                if k >= 1 and not added_by_tensor(k - 1):
+                    add_up(k - 1)
+                carried(k)
                 for e in range(PAIR):
-                    tanh(cand2[k], side2, blk, e)
+                    nc.scalar.activation(
+                        out=cand2[k][:, e, :], in_=cand2[k][:, e, :], func=ACT.Tanh,
+                        bias=bias_column(side2, 0, 2, blk, e, bias_neg), scale=-1.0,
+                    )
 
-            def transpose_back(i):
-                m, s = divmod(i, SIDES)
-                back[i] = back_psum.tile([P, PAIR, PAIR, P], F32, name="back")
-                for u in range(PAIR):
-                    k = m * PAIR + u
-                    terms = [cand2[k], mixed[k]] if added_by_tensor(k) else [mixed[k]]
+            def open_pieces(m):
+                for s in range(SIDES):
+                    pool, name = (gates2, "sums%d" % s) if m == SIDES * PASSES - 1 else (back_psum, "back")
+                    back[m * SIDES + s] = pool.tile([P, PAIR, PAIR, P], F32, name=name)
+
+            def transpose_back(m, u):
+                k = m * PAIR + u
+                terms = [kept[k], cand2[k]] if added_by_tensor(k) else [kept[k]]
+                for s in range(SIDES):
                     for e in range(PAIR):
                         for t, term in enumerate(terms):
                             nc.tensor.matmul(
-                                out=back[i][:, u, e, :],
+                                out=back[m * SIDES + s][:, u, e, :],
                                 lhsT=term[:, e, s * ROOTS : (s + 1) * ROOTS],
                                 rhs=identity[:],
                                 start=(t == 0),
@@ -502,21 +503,19 @@ def tile_decodertreernn_pa_kernel(
                 )
                 nc.sync.dma_start(out=out_rows[:, s, side2, cols], in_=leaving[:])
 
-            for k in range(count + 2):
+            for k in range(count + 1):
                 if k < count:
                     banks = gates_of_block(k)
                 m = leaving_in.get(k)
                 if m is not None:
-                    for s in range(SIDES):
-                        transpose_back(m * SIDES + s)
+                    open_pieces(m)
+                    transpose_back(m, 0)
+                    if k == count:
+                        for e in range(PAIR):
+                            renewed(k - 1, slice(e, e + 1))
+                    transpose_back(m, 1)
                 if k < count:
                     activate_block(k, banks)
-                elif k == count:
-                    halves = [slice(s * ROOTS, (s + 1) * ROOTS) for s in range(SIDES)]
-                    for nodes in halves:
-                        mix_sub2(k - 1, nodes)
-                    for nodes in halves:
-                        mix_mul2(k - 1, nodes)
                 if m is not None:
                     store_piece(m * SIDES, nc.scalar.copy)
                     store_piece(m * SIDES + 1, nc.scalar.copy if k == count - 1 else nc.vector.tensor_copy)

import concourse.mybir as mybir
from concourse.masks import make_identity

F32 = mybir.dt.float32
BF16 = mybir.dt.bfloat16
U32 = mybir.dt.uint32
U8 = mybir.dt.uint8
FP8X4 = mybir.dt.float8_e4m3fn_x4
ACT = mybir.ActivationFunctionType
ALU = mybir.AluOpType

P = 128
H = 1024
GATES = 3
SIDES = 2
PAIR = 2
ROOTS = 128
BLOCK = P * PAIR
BLOCKS = H // BLOCK
PASSES = H // (4 * P)
WORD_BLOCKS = H // BLOCK
BANK = 512
SLABS = SIDES * BLOCKS * GATES
SLAB_WORDS = PAIR * PASSES * P

PAIRS = SLABS // 2
GROUP_PAIRS = 3

FLOPS = 2 * (ROOTS + SIDES * ROOTS) * (SIDES * GATES * H) * H


def tile_decodertreernn_pa_kernel(
    tc, h_nodes, Whh_l, bih_l, bhh_l, Whh_r, bih_r, bhh_r, out
):
    nc = tc.nc

    slab_rows = [
        w.rearrange(
            "(gate g q u e) k -> gate g u q (e k)", gate=GATES, g=PASSES, q=P, u=PAIR, e=PAIR
        )
        for w in (Whh_l, Whh_r)
    ]
    out_rows = out.rearrange("b (i s s2) h -> (b i) s s2 h", s=SIDES, s2=SIDES)

    slabs = [
        (blk, side, gate)
        for blk in range(BLOCKS)
        for side, gate in ((0, 0), (0, 2), (1, 0), (1, 2), (0, 1), (1, 1))
    ]
    slab_of = {key: n for n, key in enumerate(slabs)}

    with tc.manual_schedule(), tc.tile_pool(name="keep", bufs=1) as keep:
        identity = keep.tile([P, P], F32)
        make_identity(nc, identity[:])

        w_codes = [
            keep.tile([P, SLAB_WORDS], U32, align_bytes=64, name="w_codes%d" % n) for n in range(SLABS)
        ]
        w_scales = [
            keep.tile([P, SLAB_WORDS], U8, align_bytes=64, name="w_scales%d" % n) for n in range(SLABS)
        ]
        x_codes = [
            keep.tile([P, ROOTS], U32, align_bytes=64, name="x_codes%d" % g) for g in range(PASSES)
        ]
        x_scales = [
            keep.tile([P, ROOTS], U8, align_bytes=64, name="x_scales%d" % g) for g in range(PASSES)
        ]
        c_codes = [
            keep.tile([P, SIDES * ROOTS], U32, align_bytes=64, name="c_codes%d" % g)
            for g in range(PASSES)
        ]
        c_scales = [
            keep.tile([P, SIDES * ROOTS], U8, align_bytes=64, name="c_scales%d" % g)
            for g in range(PASSES)
        ]
        c_f32 = [
            keep.tile([P, PAIR, PAIR, SIDES * ROOTS], F32, name="c_f32_%d" % g) for g in range(PASSES)
        ]
        c_grouped = [
            keep.tile([P, SIDES * ROOTS, 2 * PAIR], BF16, align_bytes=64, name="c_grouped%d" % g)
            for g in range(PASSES)
        ]
        bias = keep.tile([P, SIDES * 2 * GATES * BLOCKS * PAIR], F32)
        bias_rz = keep.tile([P, SIDES, 2 * BLOCKS * PAIR], F32)
        bias_neg = keep.tile([P, SIDES * 2 * GATES * BLOCKS * PAIR], F32)

        def bias_column(side, kind, gate, blk, e, table=bias):
            col = ((side * 2 + kind) * GATES * BLOCKS + gate * BLOCKS + blk) * PAIR + e
            return table[:, col : col + 1]

        def bias_rz_column(side, gate, blk, e):
            col = (gate * BLOCKS + blk) * PAIR + e
            return bias_rz[:, side, col : col + 1]

        def every_second_word(w):
            g, u = divmod(w, PAIR)
            return slice(g * BLOCK + u, (g + 1) * BLOCK, PAIR)

        def multiply(bank, slab, codes, scales):
            for e in range(PAIR):
                for g in range(PASSES):
                    first = (e * PASSES + g) * P
                    nc.tensor.matmul_mx(
                        out=bank[:, e, :],
                        lhsT=w_codes[slab][:, first : first + P].bitcast(FP8X4),
                        lhsT_scale=w_scales[slab][:, first : first + P],
                        rhs=codes[g][:].bitcast(FP8X4),
                        rhs_scale=scales[g][:],
                        start=(g == 0),
                        stop=(g == PASSES - 1),
                    )

        def sigmoid(gate_out, bank, side, gate, blk, e):
            nc.scalar.activation(
                out=gate_out[:, e, :], in_=bank[:, e, :], func=ACT.Sigmoid,
                bias=bias_rz_column(side, gate, blk, e), scale=1.0,
            )

        def reset_candidate(cand, bank, reset, side, blk, e):
            nc.vector.scalar_tensor_tensor(
                out=cand[:, e, :], in0=bank[:, e, :], scalar=bias_column(side, 1, 2, blk, e),
                in1=reset[:, e, :], op0=ALU.add, op1=ALU.mult,
            )

        def tanh(cand, side, blk, e):
            nc.scalar.activation(
                out=cand[:, e, :], in_=cand[:, e, :], func=ACT.Tanh,
                bias=bias_column(side, 0, 2, blk, e), scale=1.0,
            )

        with tc.tile_pool(name="raw", bufs=SLABS) as raw_pool, tc.tile_pool(
            name="once", bufs=1
        ) as once, tc.tile_pool(name="stage", bufs=4) as stage, tc.tile_pool(
            name="work1", bufs=2
        ) as work1, tc.psum_pool(name="flip", bufs=4) as flip_psum, tc.psum_pool(
            name="gates1", bufs=4
        ) as gates1:
            x_raw = once.tile([P, H], BF16)
            bias_raw = once.tile([P, PAIR * BLOCK], BF16)
            nc.vector.memset(bias_raw[:], 0.0)
            rows = GATES * PASSES
            raw = []
            for n, (blk, side, gate) in enumerate(slabs):
                raw_slab = raw_pool.tile([P, PAIR * H], BF16, name="raw_slab")
                nc.sync.dma_start(out=raw_slab[:], in_=slab_rows[side][gate, blk // PAIR, blk % PAIR])
                raw.append(raw_slab)
                if n == 0:
                    nc.sync.dma_start(out=x_raw[:], in_=h_nodes.flatten_outer_dims())

            warm = once.tile([P, 1], F32)
            nc.vector.memset(warm[:], 0.0)
            nc.scalar.activation(out=warm[:], in_=warm[:], func=ACT.Sigmoid)

            for v, vec in enumerate((bih_l, bhh_l, bih_r, bhh_r)):
                nc.scalar.dma_start(
                    out=bias_raw[v * rows : (v + 1) * rows, :],
                    in_=vec.rearrange("(r c) -> r c", c=PAIR * BLOCK),
                )

            x_grouped = once.tile([P, BANK], F32, align_bytes=64)
            flipped = {}
            grouped = {}
            sums = {}
            reset, update, cand, diff = {}, {}, {}, {}

            def transpose_slab(n):
                words = raw[n][:].bitcast(F32)
                for e in range(PAIR):
                    flipped[(n, e)] = flip_psum.tile([P, BANK], F32, name="flipped")
                    for w in range(WORD_BLOCKS):
                        nc.tensor.transpose(
                            flipped[(n, e)][:, w * P : (w + 1) * P],
                            words[:, every_second_word(e * WORD_BLOCKS + w)],
                            identity[:],
                        )

            def bring_states():
                x_words = x_raw[:].bitcast(F32)
                x_flipped = flip_psum.tile([P, BANK], F32, name="flipped")
                for w in range(WORD_BLOCKS):
                    nc.tensor.transpose(
                        x_flipped[:, w * P : (w + 1) * P], x_words[:, every_second_word(w)], identity[:]
                    )
                nc.vector.tensor_copy(
                    out=x_grouped[:].rearrange("p (g j u) -> p g j u", g=PASSES, u=PAIR),
                    in_=x_flipped[:].rearrange("p (g u j) -> p g j u", g=PASSES, u=PAIR),
                )

            def quantise_states():
                for g in range(PASSES):
                    nc.vector.quantize_mx(
                        out=x_codes[g][:].bitcast(FP8X4),
                        scales=x_scales[g][:],
                        in_=x_grouped[:, g * BLOCK : (g + 1) * BLOCK].bitcast(BF16),
                    )

            def state_values(blk):
                g, u = divmod(blk, PAIR)
                values = x_grouped[:].bitcast(BF16)[:, g * PAIR * BLOCK : (g + 1) * PAIR * BLOCK]
                return values.rearrange("p (j u e) -> p u e j", u=PAIR, e=PAIR)[:, u]

            def transpose_biases():
                b_flipped = gates1.tile([P, PAIR, P], F32, name="sums")
                bias_words = bias_raw[:].bitcast(F32)
                for u in range(PAIR):
                    nc.tensor.transpose(
                        b_flipped[:, u, :], bias_words[:, every_second_word(u)], identity[:]
                    )
                return b_flipped

            def spread_biases(b_flipped):
                nc.vector.tensor_copy(
                    out=bias[:].rearrange("p (r u e) -> p r u e", u=PAIR, e=PAIR),
                    in_=b_flipped[:].bitcast(BF16).rearrange("p u (r e) -> p r u e", e=PAIR)[
                        :, 0 : SIDES * 2 * rows
                    ],
                )
                by_kind = bias[:].rearrange("p (s kind c) -> p s kind c", s=SIDES, kind=2)
                rz_cols = 2 * BLOCKS * PAIR
                nc.vector.tensor_scalar_mul(bias_neg[:], bias[:], -1.0)
                nc.vector.tensor_add(
                    out=bias_rz[:], in0=by_kind[:, :, 0, 0:rz_cols], in1=by_kind[:, :, 1, 0:rz_cols]
                )

            def empty_bank(n, e):
                if e == 0:
                    grouped[n] = stage.tile([P, PAIR * BANK], F32, align_bytes=64, name="grouped")
                by_vector = (n % (2 * GROUP_PAIRS), e) in ((3, 1), (4, 0)) and n < SLABS - 4
                copy = nc.vector.tensor_copy if by_vector else nc.scalar.copy
                copy(
                    out=grouped[n][:, e * BANK : (e + 1) * BANK].rearrange(
                        "p (g q u) -> p g q u", g=PASSES, u=PAIR
                    ),
                    in_=flipped[(n, e)][:].rearrange("p (g u q) -> p g q u", g=PASSES, u=PAIR),
                )

            def quantise_rows(n, parities):
                cols = slice(parities[0] * BLOCK, (parities[-1] + 1) * BLOCK)
                words = slice(parities[0] * BANK, (parities[-1] + 1) * BANK)
                nc.vector.quantize_mx(
                    out=w_codes[n][:, cols].bitcast(FP8X4),
                    scales=w_scales[n][:, cols],
                    in_=grouped[n][:, words].bitcast(BF16),
                )

            def quantise_slab(n):
                quantise_rows(n, range(PAIR))

            def multiply_slab(n):
                sums[n] = gates1.tile([P, PAIR, ROOTS], F32, name="sums")
                multiply(sums[n], n, x_codes, x_scales)

            def sides_tile(tiles, name, blk):
                if blk not in tiles:
                    tiles[blk] = work1.tile([P, SIDES, PAIR, ROOTS], F32, name=name)
                return tiles[blk]

            def gate_on(gates, name, blk, side, gate):
                gate_out = sides_tile(gates, name, blk)[:, side]
                for e in range(PAIR):
                    sigmoid(gate_out, sums[slab_of[(blk, side, gate)]], side, gate, blk, e)

            def reset_on(blk, side):
                gate_on(reset, "reset", blk, side, 0)

            def update_on(blk, side):
                gate_on(update, "update", blk, side, 1)

            def candidate(blk, side):
                cand_out = sides_tile(cand, "cand", blk)[:, side]
                for e in range(PAIR):
                    reset_candidate(
                        cand_out, sums[slab_of[(blk, side, 2)]], reset[blk][:, side], side, blk, e
                    )

            def candidate_on(blk, side):
                for e in range(PAIR):
                    tanh(cand[blk][:, side], side, blk, e)

            def mix_sub(blk):
                nc.vector.tensor_sub(
                    out=sides_tile(diff, "diff", blk)[:],
                    in0=state_values(blk).unsqueeze(1).to_broadcast([P, SIDES, PAIR, ROOTS]),
                    in1=cand[blk][:],
                )

            both = slice(0, SIDES)

            def mix_mul(blk, sides):
                nc.vector.tensor_mul(
                    out=diff[blk][:, sides], in0=update[blk][:, sides], in1=diff[blk][:, sides]
                )

            def nodes_of(side):
                return slice(side * ROOTS, (side + 1) * ROOTS)

            def mix_add(blk):
                g, u = divmod(blk, PAIR)
                nc.vector.tensor_add(
                    out=c_f32[g][:, u].rearrange("p e (s j) -> p s e j", s=SIDES),
                    in0=diff[blk][:],
                    in1=cand[blk][:],
                )

            def round_states(g):
                nc.vector.tensor_copy(
                    out=c_grouped[g][:].rearrange("p j (u e) -> p j u e", u=PAIR),
                    in_=c_f32[g][:].rearrange("p u e j -> p j u e"),
                )

            def mix_round(blk, side):
                g, u = divmod(blk, PAIR)
                nc.vector.tensor_add(
                    out=c_grouped[g][:, nodes_of(side), u * PAIR : (u + 1) * PAIR],
                    in0=diff[blk][:, side].rearrange("p e j -> p j e"),
                    in1=cand[blk][:, side].rearrange("p e j -> p j e"),
                )

            def quantise_children(g, side):
                nc.vector.quantize_mx(
                    out=c_codes[g][:, nodes_of(side)].bitcast(FP8X4),
                    scales=c_scales[g][:, nodes_of(side)],
                    in_=c_grouped[g][:, nodes_of(side), :].rearrange("p c t -> p (c t)"),
                )

            last = PAIRS - 1
            for i in range(last):
                transpose_slab(2 * i)
                if i == 0:
                    bring_states()
                if i >= 1:
                    quantise_slab(2 * i - 1)
                q, turn = divmod(i - 2, GROUP_PAIRS)
                now = q >= 0
                late = q >= 1
                if turn == 0:
                    if late:
                        update_on(q - 1, 1)
                    reset_on(q, 0)
                elif turn == 1 and now:
                    reset_on(q, 1)
                elif turn == 2 and now:
                    update_on(q, 0)
                if i >= 1:
                    multiply_slab(2 * i - 2)
                empty_bank(2 * i, 0)
                empty_bank(2 * i, 1)
                transpose_slab(2 * i + 1)
                if i == 1:
                    b_flipped = transpose_biases()
                if i >= 1:
                    multiply_slab(2 * i - 1)
                if turn == 0:
                    if late:
                        mix_mul(q - 1, both)
                    candidate(q, 0)
                elif turn == 1 and now:
                    candidate_on(q, 0)
                    candidate(q, 1)
                    if q == PAIR:
                        for side in range(SIDES):
                            quantise_children(0, side)
                elif turn == 2 and now:
                    candidate_on(q, 1)
                if i == 0:
                    quantise_states()
                quantise_slab(2 * i)
                empty_bank(2 * i + 1, 0)
                empty_bank(2 * i + 1, 1)
                if turn == 0 and late:
                    mix_add(q - 1)
                    if q == PAIR:
                        round_states(0)
                elif turn == 2 and now:
                    mix_sub(q)
                if i == 1:
                    spread_biases(b_flipped)

            blk = BLOCKS - 1
            g = blk // PAIR
            left, right = 2 * last, 2 * last + 1
            transpose_slab(left)
            quantise_slab(left - 1)
            update_on(blk - 1, 1)
            reset_on(blk, 0)
            multiply_slab(left - 2)
            multiply_slab(left - 1)
            transpose_slab(right)
            mix_mul(blk - 1, both)
            candidate(blk, 0)
            empty_bank(left, 0)
            empty_bank(left, 1)
            for side in range(SIDES):
                mix_round(blk - 1, side)
            candidate_on(blk, 0)
            reset_on(blk, 1)
            quantise_slab(left)
            multiply_slab(left)
            candidate(blk, 1)
            empty_bank(right, 0)
            empty_bank(right, 1)
            candidate_on(blk, 1)
            quantise_rows(right, [0])
            update_on(blk, 0)
            quantise_rows(right, [1])
            multiply_slab(right)
            mix_sub(blk)
            mix_mul(blk, slice(0, 1))
            update_on(blk, 1)
            mix_round(blk, 0)
            mix_mul(blk, slice(1, SIDES))
            quantise_children(g, 0)
            mix_round(blk, 1)
            quantise_children(g, 1)
            mix_add(blk - 1)
            mix_add(blk)

        with tc.tile_pool(name="work2", bufs=5) as work2, tc.psum_pool(
            name="gates2", bufs=2
        ) as gates2, tc.psum_pool(name="back", bufs=2) as back_psum:
            children = SIDES * ROOTS
            blocks2 = [(side2, blk) for side2 in range(SIDES) for blk in range(BLOCKS)]
            count = len(blocks2)
            update2, cand2, kept, back = {}, {}, {}, {}
            leaving_in = {3: 0, 5: 1, 7: 2, 8: 3}

            def gates_of_block(k):
                side2, blk = blocks2[k]
                banks = {}
                for gate in (0, 2, 1):
                    banks[gate] = gates2.tile([P, PAIR, children], F32, name="sums%d" % gate)
                    multiply(banks[gate], slab_of[(blk, side2, gate)], c_codes, c_scales)
                return banks

            def carried(k):
                g, u = divmod(blocks2[k][1], PAIR)
                kept[k] = work2.tile([P, PAIR, children], F32, name="kept")
                nc.vector.tensor_mul(out=kept[k][:], in0=update2[k][:], in1=c_f32[g][:, u])

            def renewed(k, parities=slice(0, PAIR)):
                part = cand2[k][:, parities]
                nc.vector.scalar_tensor_tensor(
                    out=part, in0=update2[k][:, parities], scalar=1.0, in1=part,
                    op0=ALU.subtract, op1=ALU.mult,
                )

            def added_by_tensor(k):
                return k >= count // 2

            def add_up(k):
                nc.vector.tensor_add(out=kept[k][:], in0=kept[k][:], in1=cand2[k][:])

            def activate_block(k, banks):
                side2, blk = blocks2[k]
                reset2 = work2.tile([P, PAIR, children], F32)
                update2[k] = work2.tile([P, PAIR, children], F32, name="update2")
                cand2[k] = work2.tile([P, PAIR, children], F32, name="cand2")
                for e in range(PAIR):
                    sigmoid(reset2, banks[0], side2, 0, blk, e)
                if k >= 1:
                    renewed(k - 1)
                for e in range(PAIR):
                    reset_candidate(cand2[k], banks[2], reset2, side2, blk, e)
                for e in range(PAIR):
                    sigmoid(update2[k], banks[1], side2, 1, blk, e)
                if k >= 1 and not added_by_tensor(k - 1):
                    add_up(k - 1)
                carried(k)
                for e in range(PAIR):
                    nc.scalar.activation(
                        out=cand2[k][:, e, :], in_=cand2[k][:, e, :], func=ACT.Tanh,
                        bias=bias_column(side2, 0, 2, blk, e, bias_neg), scale=-1.0,
                    )

            def open_pieces(m):
                for s in range(SIDES):
                    pool, name = (gates2, "sums%d" % s) if m == SIDES * PASSES - 1 else (back_psum, "back")
                    back[m * SIDES + s] = pool.tile([P, PAIR, PAIR, P], F32, name=name)

            def transpose_back(m, u):
                k = m * PAIR + u
                terms = [kept[k], cand2[k]] if added_by_tensor(k) else [kept[k]]
                for s in range(SIDES):
                    for e in range(PAIR):
                        for t, term in enumerate(terms):
                            nc.tensor.matmul(
                                out=back[m * SIDES + s][:, u, e, :],
                                lhsT=term[:, e, s * ROOTS : (s + 1) * ROOTS],
                                rhs=identity[:],
                                start=(t == 0),
                                stop=(t == len(terms) - 1),
                                is_transpose=True,
                            )

            def store_piece(i, copy):
                m, s = divmod(i, SIDES)
                side2, g = divmod(m, PASSES)
                cols = slice(g * PAIR * BLOCK, (g + 1) * PAIR * BLOCK)
                leaving = work2.tile([P, PAIR * BLOCK], F32)
                copy(
                    out=leaving[:].rearrange("j (q u e) -> j q u e", u=PAIR, e=PAIR),
                    in_=back[i][:].rearrange("j u e q -> j q u e"),
                )
                nc.sync.dma_start(out=out_rows[:, s, side2, cols], in_=leaving[:])

            for k in range(count + 1):
                if k < count:
                    banks = gates_of_block(k)
                m = leaving_in.get(k)
                if m is not None:
                    open_pieces(m)
                    transpose_back(m, 0)
                    if k == count:
                        for e in range(PAIR):
                            renewed(k - 1, slice(e, e + 1))
                    transpose_back(m, 1)
                if k < count:
                    activate_block(k, banks)
                if m is not None:
                    store_piece(m * SIDES, nc.scalar.copy)
                    store_piece(m * SIDES + 1, nc.scalar.copy if k == count - 1 else nc.vector.tensor_copy)
